import numpy as np
import ml_dtypes


def mxq(x, axis, fmt="e4m3"):
    dtype, down = {"e4m3": (ml_dtypes.float8_e4m3fn, 7), "e5m2": (ml_dtypes.float8_e5m2, 14)}[fmt]
    v = np.moveaxis(np.asarray(x, np.float32).astype(ml_dtypes.bfloat16).astype(np.float64), axis, -1)
    blocks = v.reshape(v.shape[:-1] + (-1, 32))
    amax = np.abs(blocks).max(-1, keepdims=True)
    byte = np.maximum(np.where(amax > 0, np.frexp(amax)[1] - 1 + 127, 0) - down, 1)
    scale = np.exp2(byte - 127.0)
    codes = (blocks / scale).astype(np.float32).astype(dtype).astype(np.float64)
    return np.moveaxis((codes * scale).reshape(v.shape), -1, axis)


WIDE = False


def mx_kscale(k):
    if not WIDE:
        return np.ones(k)
    levels = np.array([10, -10, 5, -5, 0])
    a = np.random.permutation(np.resize(levels, k // 512 * 4)).reshape(k // 512, 4)
    idx = np.arange(k)
    return np.exp2(a[idx // 512, idx % 128 // 32])


BF16 = ml_dtypes.bfloat16


def bf(x):
    return np.asarray(x, np.float32).astype(BF16)


def f64(x):
    return np.asarray(x).astype(np.float64)


E2M1 = np.array([0.0, 0.5, 1.0, 1.5, 2.0, 3.0, 4.0, 6.0, -0.0, -0.5, -1.0, -1.5, -2.0, -3.0, -4.0, -6.0])


def pack_weight(w, fmt):
    k, n = w.shape
    w = f64(bf(w)).reshape(k // 32, 32, n)
    amax = np.abs(w).max(1)
    if fmt == "e4m3":
        byte = np.frexp(amax)[1] - 1 + 127 - 7
    else:
        mant, ex = np.frexp(amax / 6.0)
        byte = np.where(mant > 0.5, ex, ex - 1) + 127
    byte = np.clip(np.where(amax > 0, byte, 1), 1, 254)
    scaled = (w * np.exp2(127.0 - byte)[:, None, :]).reshape(k, n).astype(np.float32)
    by_word = np.ascontiguousarray(scaled.reshape(k // 512, 128, 4, n).transpose(0, 1, 3, 2))
    if fmt == "e4m3":
        words = by_word.astype(ml_dtypes.float8_e4m3fn).view(np.uint8)
    else:
        c = by_word.astype(ml_dtypes.float4_e2m1fn).view(np.uint8) & 0xF
        words = c[..., 0::2] | (c[..., 1::2] << 4)
    return np.ascontiguousarray(words), np.ascontiguousarray(byte.astype(np.uint8).reshape(k // 512, 16, n))


def unpack_weight(words, scales, fmt):
    g, p, n, _ = words.shape
    if fmt == "e4m3":
        vals = np.ascontiguousarray(words).view(ml_dtypes.float8_e4m3fn).astype(np.float64)
    else:
        nib = np.empty((g, p, n, 4), np.uint8)
        nib[..., 0::2] = words & 0xF
        nib[..., 1::2] = words >> 4
        vals = E2M1[nib]
    vals = vals * np.repeat(np.exp2(scales.astype(np.float64) - 127.0), 8, axis=1)[..., None]
    return vals.transpose(0, 1, 3, 2).reshape(g * 512, n)


B, N, F_NODE, F_EDGE, H = 8, 32, 64, 32, 512
FMT = "e4m3"


def setup_inputs():
    s, t = mx_kscale(H), mx_kscale(H)
    w1 = np.random.standard_normal((3 * H, H)) / np.sqrt(3 * H) * t
    w1[2 * H:] = w1[2 * H:] / s[:, None]
    h = bf(np.random.standard_normal((B, N, H)))
    e = bf(np.random.standard_normal((B, N, N, H)) * s)
    adj_mask = bf(np.random.uniform(size=(B, N, N, 1)) < 0.5)
    w1_words, w1_scales = pack_weight(w1, FMT)
    b_m1 = bf(np.random.standard_normal(H) * 0.3 * t)
    w2_words, w2_scales = pack_weight(np.random.standard_normal((H, H)) * 2.0 / np.sqrt(H * N) / t[:, None], FMT)
    b_m2 = bf(np.random.standard_normal(H) * 0.4 / np.sqrt(N))
    return {"h": h,
            "e": e,
            "adj_mask": adj_mask,
            "W_m1_words": w1_words,
            "W_m1_scales": w1_scales,
            "b_m1": b_m1,
            "W_m2_words": w2_words,
            "W_m2_scales": w2_scales,
            "b_m2": b_m2}


def reference(h, e, adj_mask, W_m1_words, W_m1_scales, b_m1, W_m2_words, W_m2_scales, b_m2):
    h = f64(h)
    w1 = unpack_weight(W_m1_words, W_m1_scales, FMT)
    hq = mxq(h, 2, "e4m3")
    a_i = hq @ w1[:H]
    a_j = hq @ w1[H:2 * H]
    a_e = mxq(f64(e), 3, "e4m3") @ w1[2 * H:]
    m = a_i[:, :, None, :] + a_j[:, None, :, :] + a_e + f64(b_m1)
    m = np.maximum(m, 0.0)
    m = (mxq(m, 3, "e4m3") @ unpack_weight(W_m2_words, W_m2_scales, FMT)) + f64(b_m2)
    m = m * f64(adj_mask)
    return m.sum(axis=-2) + h

@@ -1,0 +1,320 @@
+from contextlib import ExitStack
+
+import concourse.mybir as mybir
+from concourse.masks import make_identity
+
+F32 = mybir.dt.float32
+BF16 = mybir.dt.bfloat16
+I32 = mybir.dt.int32
+U32 = mybir.dt.uint32
+U8 = mybir.dt.uint8
+FP8X4 = mybir.dt.float8_e4m3fn_x4
+ADD = mybir.AluOpType.add
+MULT = mybir.AluOpType.mult
+RELU = mybir.ActivationFunctionType.Relu
+COPY = mybir.ActivationFunctionType.Copy
+
+GRAPHS = 8
+NODES = 32
+H = 512
+P = 128
+PACK = 4
+HALVES = GRAPHS * NODES // P
+GRAPHS_PER_HALF = GRAPHS // HALVES
+PAIR = 2
+ROUNDS_PER_HALF = NODES // PAIR
+ROUNDS = HALVES * ROUNDS_PER_HALF
+E_CHUNK = 4
+SPREAD_CHUNK = 8
+W_XI = 0
+W_XJ = 1
+W_E2 = 2
+W_M2 = 3
+
+FLOPS = 2 * H * H * (2 * GRAPHS * NODES * NODES + 2 * GRAPHS * NODES)
+
+
+def tile_messagepassing_pa_t_kernel(
+    tc, h, e, adj_mask, w_m1_words, w_m1_scales, b_m1, w_m2_words, w_m2_scales, b_m2, out
+):
+    nc = tc.nc
+    h_rows = h.rearrange("b i k -> (b i) k")
+    e_rows = e.rearrange("b i j k -> (b i) j k")
+    mask_rows = adj_mask.rearrange("b i j o -> (b i) (j o)")
+    out_rows = out.rearrange("b i n -> (b i) n")
+
+    with ExitStack() as ctx:
+        keep = ctx.enter_context(tc.tile_pool(name="keep", bufs=1))
+        e_pool = ctx.enter_context(tc.tile_pool(name="e_pool", bufs=HALVES * NODES // E_CHUNK))
+        spread = ctx.enter_context(tc.tile_pool(name="spread", bufs=2))
+        work = ctx.enter_context(tc.tile_pool(name="work", bufs=3))
+        sums = ctx.enter_context(tc.tile_pool(name="sums", bufs=2))
+        psum = ctx.enter_context(tc.psum_pool(name="psum", bufs=2))
+
+        w_planes = keep.tile([P, 4, H], U8, align_bytes=64)
+        nc.vector.memset(w_planes[:].bitcast(I32), 0)
+        h_sb = keep.tile([P, HALVES, H], BF16)
+        nc.sync.dma_start(out=h_sb[:], in_=h_rows.rearrange("(s p) k -> p s k", p=P))
+        for quad in range(4):
+            live = slice(32 * quad, 32 * quad + 4)
+            rows = slice(4 * quad, 4 * quad + 4)
+            nc.sync.dma_start(
+                out=w_planes[live, W_XI : W_E2 + 1, :].bitcast(I32),
+                in_=w_m1_scales[:, rows, :].bitcast(I32).rearrange("g r n -> r g n"),
+            )
+            nc.sync.dma_start(
+                out=w_planes[live, W_M2, :].bitcast(I32), in_=w_m2_scales[0, rows, :].bitcast(I32)
+            )
+        w_words = keep.tile([P, 4, H], U32, align_bytes=64)
+        nc.sync.dma_start(
+            out=w_words[:, W_XI : W_E2 + 1, :].bitcast(I32),
+            in_=w_m1_words.rearrange("g p n t -> p g (n t)").bitcast(I32),
+        )
+        e_chunks = []
+        for c in range(HALVES * NODES // E_CHUNK):
+            half, first_j = divmod(c * E_CHUNK, NODES)
+            e_sb = e_pool.tile([P, E_CHUNK, H], BF16)
+            nc.sync.dma_start(
+                out=e_sb[:], in_=e_rows[half * P : (half + 1) * P, first_j : first_j + E_CHUNK, :]
+            )
+            e_chunks.append(e_sb)
+            if c == 0:
+                nc.sync.dma_start(
+                    out=w_words[:, W_M2, :].bitcast(I32),
+                    in_=w_m2_words[0].rearrange("p n t -> p (n t)").bitcast(I32),
+                )
+        mask_bf = keep.tile([P, HALVES, NODES], BF16)
+        nc.scalar.dma_start(out=mask_bf[:], in_=mask_rows.rearrange("(s p) j -> p s j", p=P))
+        b1_all = keep.tile([P, H], BF16)
+        nc.scalar.dma_start(out=b1_all[:], in_=b_m1.partition_broadcast(P))
+        b2_all = keep.tile([P, H], BF16)
+        nc.scalar.dma_start(out=b2_all[:], in_=b_m2.partition_broadcast(P))
+
+        ident_f32 = keep.tile([P, P], F32)
+        make_identity(nc, ident_f32[:])
+
+        def words_onto_partitions(sources, grouped):
+            flipped = psum.tile([P, PAIR, 2, P], F32, tag="flipped")
+            for s in range(PAIR):
+                words = sources[s].bitcast(F32)
+                for u in range(2):
+                    nc.tensor.transpose(flipped[:, s, u, :], words[:, u : H // 2 : 2], ident_f32[:])
+            nc.scalar.copy(
+                out=grouped[:].bitcast(F32), in_=flipped[:].rearrange("p s u r -> p s r u")
+            )
+
+        def quantise(grouped, codes, scales):
+            nc.vector.quantize_mx(
+                out=codes[:].bitcast(FP8X4),
+                scales=scales[:],
+                in_=grouped[:].rearrange("p s r t -> p (s r t)"),
+            )
+
+        def mx_pass(acc, codes, scales, weight, start, stop):
+            nc.tensor.matmul_mx(
+                out=acc[:],
+                lhsT=codes.bitcast(FP8X4),
+                lhsT_scale=scales,
+                rhs=w_words[:, weight, :].bitcast(FP8X4),
+                rhs_scale=w_planes[:, weight, :],
+                start=start,
+                stop=stop,
+            )
+
+        h_grouped = keep.tile([P, HALVES, P, PACK], BF16, align_bytes=64)
+        words_onto_partitions([h_sb[:, 0, :], h_sb[:, 1, :]], h_grouped)
+        h_codes = keep.tile([P, HALVES * P], U32, align_bytes=64)
+        h_scales = keep.tile([P, HALVES * P], U8, align_bytes=64)
+        quantise(h_grouped, h_codes, h_scales)
+
+        h_fourfold = keep.tile([P, HALVES * P, 4, PACK], BF16, align_bytes=64)
+        nc.vector.tensor_copy(
+            out=h_fourfold[:],
+            in_=h_grouped[:]
+            .rearrange("p s r t -> p (s r) t")
+            .unsqueeze(2)
+            .to_broadcast([P, HALVES * P, 4, PACK]),
+        )
+        h4_codes = keep.tile([P, HALVES * P * 4], U32, align_bytes=64)
+        h4_scales = keep.tile([P, HALVES * P * 4], U8, align_bytes=64)
+        nc.vector.memset(h4_scales[:].bitcast(I32), 0)
+        nc.vector.quantize_mx(
+            out=h4_codes[:].bitcast(FP8X4),
+            scales=h4_scales[:],
+            in_=h_fourfold[:].rearrange("p c f t -> p (c f t)"),
+        )
+        h4_code_of = h4_codes[:].bitcast(I32).rearrange(
+            "p (s b j f) -> p s j b f", s=HALVES, b=GRAPHS_PER_HALF, j=NODES
+        )
+        h4_scale_of = h4_scales[:].bitcast(I32).rearrange(
+            "p (s b j) -> p s j b", s=HALVES, b=GRAPHS_PER_HALF
+        )
+
+        def spread_source_nodes(half, first_j):
+            js = slice(first_j, first_j + SPREAD_CHUNK)
+            codes = spread.tile([P, SPREAD_CHUNK, P], U32, tag="spread_codes", align_bytes=64)
+            nc.vector.tensor_copy(
+                out=codes[:].bitcast(I32).rearrange("p j (b i) -> p j b i", b=GRAPHS_PER_HALF),
+                in_=h4_code_of[:, half, js, :, 0]
+                .unsqueeze(3)
+                .to_broadcast([P, SPREAD_CHUNK, GRAPHS_PER_HALF, NODES]),
+            )
+            scales = spread.tile([P, SPREAD_CHUNK, P], U8, tag="spread_scales", align_bytes=64)
+            nc.vector.tensor_copy(
+                out=scales[:].bitcast(I32).rearrange("p j (b w) -> p j b w", b=GRAPHS_PER_HALF),
+                in_=h4_scale_of[:, half, js, :]
+                .unsqueeze(3)
+                .to_broadcast([P, SPREAD_CHUNK, GRAPHS_PER_HALF, NODES // 4]),
+            )
+            return codes, scales
+
+        mask_f32 = keep.tile([P, HALVES, NODES], F32)
+        nc.vector.tensor_copy(out=mask_f32[:], in_=mask_bf[:])
+        degree = keep.tile([P, HALVES], F32)
+        nc.vector.tensor_reduce(out=degree[:], in_=mask_f32[:], axis=mybir.AxisListType.X, op=ADD)
+
+        target_term = []
+        for half in range(HALVES):
+            cols = slice(half * P, (half + 1) * P)
+            a_i = psum.tile([P, H], F32, tag="pre")
+            mx_pass(a_i, h_codes[:, cols], h_scales[:, cols], W_XI, True, True)
+            table = keep.tile([P, 2, P, 2], F32, name="target_term%d" % half)
+            nc.vector.tensor_tensor(
+                out=table[:],
+                in0=a_i[:].rearrange("r (p u v) -> r u p v", u=2, v=2),
+                in1=b1_all[:].rearrange("r (p u v) -> r u p v", u=2, v=2),
+                op=ADD,
+            )
+            target_term.append(table)
+
+        e_quantised = {}
+        spread_h = {}
+        pre_rounded = {}
+        r_quantised = {}
+        running = {}
+
+        def half_and_j(rnd):
+            half, pair = divmod(rnd, ROUNDS_PER_HALF)
+            return half, pair * PAIR
+
+        def flip_e(rnd):
+            half, j = half_and_j(rnd)
+            chunk = e_chunks[(half * NODES + j) // E_CHUNK]
+            grouped = work.tile([P, PAIR, P, PACK], BF16, tag="e_grouped", align_bytes=64)
+            words_onto_partitions([chunk[:, (j + s) % E_CHUNK, :] for s in range(PAIR)], grouped)
+            return grouped
+
+        def quantise_pair(grouped, tag):
+            codes = work.tile([P, PAIR * P], U32, tag=tag + "_codes", align_bytes=64)
+            scales = work.tile([P, PAIR * P], U8, tag=tag + "_scales", align_bytes=64)
+            quantise(grouped, codes, scales)
+            return codes, scales
+
+        def first_layer(rnd):
+            half, j = half_and_j(rnd)
+            codes, scales = e_quantised[rnd]
+            h_spread_codes, h_spread_scales = spread_h[(half, j // SPREAD_CHUNK)]
+            rounded = []
+            for s in range(PAIR):
+                cols = slice(s * P, (s + 1) * P)
+                pre = psum.tile([P, H], F32, tag="pre")
+                mx_pass(pre, codes[:, cols], scales[:, cols], W_E2, True, False)
+                mx_pass(
+                    pre,
+                    h_spread_codes[:, (j + s) % SPREAD_CHUNK, :],
+                    h_spread_scales[:, (j + s) % SPREAD_CHUNK, :],
+                    W_XJ,
+                    False,
+                    True,
+                )
+                p_bf = work.tile([P, 2, P, 2], BF16, tag="p_bf", bufs=2 * PAIR)
+                nc.vector.tensor_tensor(
+                    out=p_bf[:],
+                    in0=pre[:].rearrange("r (p u v) -> r u p v", u=2, v=2),
+                    in1=target_term[half][:],
+                    op=ADD,
+                )
+                rounded.append(p_bf)
+            pre_rounded[rnd] = rounded
+
+        def flip_r(rnd):
+            rounded = pre_rounded[rnd]
+            flipped = psum.tile([P, 2, PAIR * P], F32, tag="r_flipped")
+            for s in range(PAIR):
+                words = rounded[s][:].rearrange("r u p v -> r (u p v)").bitcast(F32)
+                for u in range(2):
+                    nc.tensor.transpose(
+                        flipped[:, u, s * P : (s + 1) * P], words[:, u * P : (u + 1) * P], ident_f32[:]
+                    )
+            grouped = work.tile([P, PAIR, P, PACK], BF16, tag="r_grouped", align_bytes=64)
+            nc.scalar.activation(
+                out=grouped[:].rearrange("p s r (u v) -> p (s r) u v", u=2),
+                in_=flipped[:].bitcast(BF16).rearrange("p u (c v) -> p c u v", v=2),
+                func=RELU,
+            )
+            return grouped
+
+        def second_layer(rnd):
+            half, j = half_and_j(rnd)
+            codes, scales = r_quantised[rnd]
+            for s in range(PAIR):
+                cols = slice(s * P, (s + 1) * P)
+                message = psum.tile([P, H], F32, tag="message")
+                mx_pass(message, codes[:, cols], scales[:, cols], W_M2, True, True)
+                mask_j = mask_f32[:, half, j + s : j + s + 1]
+                if s == 0:
+                    nc.vector.scalar_tensor_tensor(
+                        out=running[half][s][:],
+                        in0=message[:],
+                        scalar=mask_j,
+                        in1=running[half][s][:],
+                        op0=MULT,
+                        op1=ADD,
+                    )
+                else:
+                    masked = work.tile([P, H], F32, tag="masked")
+                    nc.scalar.activation(out=masked[:], in_=message[:], func=COPY, scale=mask_j)
+                    nc.gpsimd.tensor_tensor(
+                        out=running[half][s][:], in0=running[half][s][:], in1=masked[:], op=ADD
+                    )
+
+        def start_sums(half):
+            even = sums.tile([P, H], F32, tag="even")
+            nc.vector.scalar_tensor_tensor(
+                out=even[:],
+                in0=b2_all[:],
+                scalar=degree[:, half : half + 1],
+                in1=h_sb[:, half, :],
+                op0=MULT,
+                op1=ADD,
+            )
+            odd = sums.tile([P, H], F32, tag="odd")
+            nc.gpsimd.memset(odd[:], 0.0)
+            running[half] = [even, odd]
+
+        def store_half(half):
+            even, odd = running[half]
+            nc.vector.tensor_tensor(out=even[:], in0=even[:], in1=odd[:], op=ADD)
+            nc.sync.dma_start(out=out_rows[half * P : (half + 1) * P, :], in_=even[:])
+
+        for now in range(-1, ROUNDS + 2):
+            ahead, behind, last = now + 1, now - 1, now - 2
+            if ahead < ROUNDS:
+                e_grouped = flip_e(ahead)
+            if 0 <= behind < ROUNDS:
+                r_grouped = flip_r(behind)
+            if ahead < ROUNDS:
+                e_quantised[ahead] = quantise_pair(e_grouped, "e")
+                half, j = half_and_j(ahead)
+                if j % SPREAD_CHUNK == 0:
+                    spread_h[(half, j // SPREAD_CHUNK)] = spread_source_nodes(half, j)
+                if j == 0:
+                    start_sums(half)
+            if 0 <= now < ROUNDS:
+                first_layer(now)
+            if 0 <= behind < ROUNDS:
+                r_quantised[behind] = quantise_pair(r_grouped, "r")
+            if 0 <= last < ROUNDS:
+                second_layer(last)
+                if (last + 1) % ROUNDS_PER_HALF == 0:
+                    store_half(last // ROUNDS_PER_HALF)

@@ -22,9 +22,10 @@ PACK = 4
 HALVES = GRAPHS * NODES // P
 GRAPHS_PER_HALF = GRAPHS // HALVES
 PAIR = 2
-ROUNDS_PER_HALF = NODES // PAIR
+ROUND_PAIRS = 2
+ROUND_BLOCKS = ROUND_PAIRS * PAIR
+ROUNDS_PER_HALF = NODES // ROUND_BLOCKS
 ROUNDS = HALVES * ROUNDS_PER_HALF
-E_CHUNK = 4
 SPREAD_CHUNK = 8
 W_XI = 0
 W_XJ = 1
@@ -45,11 +46,12 @@ def tile_messagepassing_pa_t_kernel(
 
     with ExitStack() as ctx:
         keep = ctx.enter_context(tc.tile_pool(name="keep", bufs=1))
-        e_pool = ctx.enter_context(tc.tile_pool(name="e_pool", bufs=HALVES * NODES // E_CHUNK))
+        e_pool = ctx.enter_context(tc.tile_pool(name="e_pool", bufs=ROUNDS))
         spread = ctx.enter_context(tc.tile_pool(name="spread", bufs=2))
-        work = ctx.enter_context(tc.tile_pool(name="work", bufs=3))
+        work = ctx.enter_context(tc.tile_pool(name="work", bufs=2 * ROUND_PAIRS))
         sums = ctx.enter_context(tc.tile_pool(name="sums", bufs=2))
         psum = ctx.enter_context(tc.psum_pool(name="psum", bufs=2))
+        ctx.enter_context(tc.manual_schedule())
 
         w_planes = keep.tile([P, 4, H], U8, align_bytes=64)
         nc.vector.memset(w_planes[:].bitcast(I32), 0)
@@ -70,45 +72,55 @@ def tile_messagepassing_pa_t_kernel(
             out=w_words[:, W_XI : W_E2 + 1, :].bitcast(I32),
             in_=w_m1_words.rearrange("g p n t -> p g (n t)").bitcast(I32),
         )
-        e_chunks = []
-        for c in range(HALVES * NODES // E_CHUNK):
-            half, first_j = divmod(c * E_CHUNK, NODES)
-            e_sb = e_pool.tile([P, E_CHUNK, H], BF16)
+        e_of_round = []
+        for rnd in range(ROUNDS):
+            half, first_j = divmod(rnd * ROUND_BLOCKS, NODES)
+            e_sb = e_pool.tile([P, ROUND_BLOCKS, H], BF16)
             nc.sync.dma_start(
-                out=e_sb[:], in_=e_rows[half * P : (half + 1) * P, first_j : first_j + E_CHUNK, :]
+                out=e_sb[:],
+                in_=e_rows[half * P : (half + 1) * P, first_j : first_j + ROUND_BLOCKS, :],
             )
-            e_chunks.append(e_sb)
-            if c == 0:
+            e_of_round.append(e_sb)
+            if rnd == 0:
                 nc.sync.dma_start(
                     out=w_words[:, W_M2, :].bitcast(I32),
                     in_=w_m2_words[0].rearrange("p n t -> p (n t)").bitcast(I32),
                 )
-        mask_bf = keep.tile([P, HALVES, NODES], BF16)
-        nc.scalar.dma_start(out=mask_bf[:], in_=mask_rows.rearrange("(s p) j -> p s j", p=P))
         b1_all = keep.tile([P, H], BF16)
         nc.scalar.dma_start(out=b1_all[:], in_=b_m1.partition_broadcast(P))
+        mask_bf = keep.tile([P, HALVES, NODES], BF16)
+        nc.scalar.dma_start(out=mask_bf[:], in_=mask_rows.rearrange("(s p) j -> p s j", p=P))
         b2_all = keep.tile([P, H], BF16)
         nc.scalar.dma_start(out=b2_all[:], in_=b_m2.partition_broadcast(P))
 
-        ident_f32 = keep.tile([P, P], F32)
-        make_identity(nc, ident_f32[:])
+        ident = keep.tile([P, P], F32)
+        make_identity(nc, ident[:])
 
-        def words_onto_partitions(sources, grouped):
-            flipped = psum.tile([P, PAIR, 2, P], F32, tag="flipped")
+        def flip_input_pair(sources):
+            flipped = psum.tile([P, 2, PAIR * P], F32, tag="flipped")
             for s in range(PAIR):
                 words = sources[s].bitcast(F32)
                 for u in range(2):
-                    nc.tensor.transpose(flipped[:, s, u, :], words[:, u : H // 2 : 2], ident_f32[:])
-            nc.scalar.copy(
-                out=grouped[:].bitcast(F32), in_=flipped[:].rearrange("p s u r -> p s r u")
-            )
+                    nc.tensor.transpose(
+                        flipped[:, u, s * P : (s + 1) * P], words[:, u : H // 2 : 2], ident[:]
+                    )
+            return flipped
+
+        def group_words(flipped, grouped):
+            nc.scalar.copy(out=grouped[:].bitcast(F32), in_=flipped[:].rearrange("p u c -> p c u"))
 
         def quantise(grouped, codes, scales):
             nc.vector.quantize_mx(
                 out=codes[:].bitcast(FP8X4),
                 scales=scales[:],
-                in_=grouped[:].rearrange("p s r t -> p (s r t)"),
+                in_=grouped[:].rearrange("p c t -> p (c t)"),
             )
+
+        def quantise_pair(grouped, tag):
+            codes = work.tile([P, PAIR * P], U32, tag=tag + "_codes", align_bytes=64)
+            scales = work.tile([P, PAIR * P], U8, tag=tag + "_scales", align_bytes=64)
+            quantise(grouped, codes, scales)
+            return codes, scales
 
         def mx_pass(acc, codes, scales, weight, start, stop):
             nc.tensor.matmul_mx(
@@ -121,60 +133,37 @@ def tile_messagepassing_pa_t_kernel(
                 stop=stop,
             )
 
-        h_grouped = keep.tile([P, HALVES, P, PACK], BF16, align_bytes=64)
-        words_onto_partitions([h_sb[:, 0, :], h_sb[:, 1, :]], h_grouped)
+        h_grouped = keep.tile([P, HALVES * P, PACK], BF16, align_bytes=64)
+        group_words(flip_input_pair([h_sb[:, 0, :], h_sb[:, 1, :]]), h_grouped)
         h_codes = keep.tile([P, HALVES * P], U32, align_bytes=64)
         h_scales = keep.tile([P, HALVES * P], U8, align_bytes=64)
         quantise(h_grouped, h_codes, h_scales)
-
-        h_fourfold = keep.tile([P, HALVES * P, 4, PACK], BF16, align_bytes=64)
-        nc.vector.tensor_copy(
-            out=h_fourfold[:],
-            in_=h_grouped[:]
-            .rearrange("p s r t -> p (s r) t")
-            .unsqueeze(2)
-            .to_broadcast([P, HALVES * P, 4, PACK]),
-        )
-        h4_codes = keep.tile([P, HALVES * P * 4], U32, align_bytes=64)
-        h4_scales = keep.tile([P, HALVES * P * 4], U8, align_bytes=64)
-        nc.vector.memset(h4_scales[:].bitcast(I32), 0)
-        nc.vector.quantize_mx(
-            out=h4_codes[:].bitcast(FP8X4),
-            scales=h4_scales[:],
-            in_=h_fourfold[:].rearrange("p c f t -> p (c f t)"),
-        )
-        h4_code_of = h4_codes[:].bitcast(I32).rearrange(
-            "p (s b j f) -> p s j b f", s=HALVES, b=GRAPHS_PER_HALF, j=NODES
-        )
-        h4_scale_of = h4_scales[:].bitcast(I32).rearrange(
-            "p (s b j) -> p s j b", s=HALVES, b=GRAPHS_PER_HALF
-        )
-
-        def spread_source_nodes(half, first_j):
-            js = slice(first_j, first_j + SPREAD_CHUNK)
-            codes = spread.tile([P, SPREAD_CHUNK, P], U32, tag="spread_codes", align_bytes=64)
-            nc.vector.tensor_copy(
-                out=codes[:].bitcast(I32).rearrange("p j (b i) -> p j b i", b=GRAPHS_PER_HALF),
-                in_=h4_code_of[:, half, js, :, 0]
-                .unsqueeze(3)
-                .to_broadcast([P, SPREAD_CHUNK, GRAPHS_PER_HALF, NODES]),
-            )
-            scales = spread.tile([P, SPREAD_CHUNK, P], U8, tag="spread_scales", align_bytes=64)
-            nc.vector.tensor_copy(
-                out=scales[:].bitcast(I32).rearrange("p j (b w) -> p j b w", b=GRAPHS_PER_HALF),
-                in_=h4_scale_of[:, half, js, :]
-                .unsqueeze(3)
-                .to_broadcast([P, SPREAD_CHUNK, GRAPHS_PER_HALF, NODES // 4]),
-            )
-            return codes, scales
-
         mask_f32 = keep.tile([P, HALVES, NODES], F32)
-        nc.vector.tensor_copy(out=mask_f32[:], in_=mask_bf[:])
         degree = keep.tile([P, HALVES], F32)
-        nc.vector.tensor_reduce(out=degree[:], in_=mask_f32[:], axis=mybir.AxisListType.X, op=ADD)
 
-        target_term = []
-        for half in range(HALVES):
+        target_term = {}
+        fourfold = {}
+        running = {}
+        spread_h = {}
+
+        def repeat_h(half):
+            cols = slice(half * P, (half + 1) * P)
+            repeated = keep.tile([P, P, 4, PACK], BF16, name="repeated%d" % half, align_bytes=64)
+            nc.scalar.copy(
+                out=repeated[:].bitcast(F32),
+                in_=h_grouped[:, cols, :].bitcast(F32).unsqueeze(2).to_broadcast([P, P, 4, 2]),
+            )
+            codes = keep.tile([P, P * 4], U32, name="fourfold_codes%d" % half, align_bytes=64)
+            scales = keep.tile([P, P * 4], U8, name="fourfold_scales%d" % half, align_bytes=64)
+            nc.vector.memset(scales[:].bitcast(I32), 0)
+            nc.vector.quantize_mx(
+                out=codes[:].bitcast(FP8X4),
+                scales=scales[:],
+                in_=repeated[:].rearrange("p c f t -> p (c f t)"),
+            )
+            fourfold[half] = (codes, scales)
+
+        def start_half(half):
             cols = slice(half * P, (half + 1) * P)
             a_i = psum.tile([P, H], F32, tag="pre")
             mx_pass(a_i, h_codes[:, cols], h_scales[:, cols], W_XI, True, True)
@@ -185,100 +174,15 @@ def tile_messagepassing_pa_t_kernel(
                 in1=b1_all[:].rearrange("r (p u v) -> r u p v", u=2, v=2),
                 op=ADD,
             )
-            target_term.append(table)
+            target_term[half] = table
 
-        e_quantised = {}
-        spread_h = {}
-        pre_rounded = {}
-        r_quantised = {}
-        running = {}
-
-        def half_and_j(rnd):
-            half, pair = divmod(rnd, ROUNDS_PER_HALF)
-            return half, pair * PAIR
-
-        def flip_e(rnd):
-            half, j = half_and_j(rnd)
-            chunk = e_chunks[(half * NODES + j) // E_CHUNK]
-            grouped = work.tile([P, PAIR, P, PACK], BF16, tag="e_grouped", align_bytes=64)
-            words_onto_partitions([chunk[:, (j + s) % E_CHUNK, :] for s in range(PAIR)], grouped)
-            return grouped
-
-        def quantise_pair(grouped, tag):
-            codes = work.tile([P, PAIR * P], U32, tag=tag + "_codes", align_bytes=64)
-            scales = work.tile([P, PAIR * P], U8, tag=tag + "_scales", align_bytes=64)
-            quantise(grouped, codes, scales)
-            return codes, scales
-
-        def first_layer(rnd):
-            half, j = half_and_j(rnd)
-            codes, scales = e_quantised[rnd]
-            h_spread_codes, h_spread_scales = spread_h[(half, j // SPREAD_CHUNK)]
-            rounded = []
-            for s in range(PAIR):
-                cols = slice(s * P, (s + 1) * P)
-                pre = psum.tile([P, H], F32, tag="pre")
-                mx_pass(pre, codes[:, cols], scales[:, cols], W_E2, True, False)
-                mx_pass(
-                    pre,
-                    h_spread_codes[:, (j + s) % SPREAD_CHUNK, :],
-                    h_spread_scales[:, (j + s) % SPREAD_CHUNK, :],
-                    W_XJ,
-                    False,
-                    True,
-                )
-                p_bf = work.tile([P, 2, P, 2], BF16, tag="p_bf", bufs=2 * PAIR)
-                nc.vector.tensor_tensor(
-                    out=p_bf[:],
-                    in0=pre[:].rearrange("r (p u v) -> r u p v", u=2, v=2),
-                    in1=target_term[half][:],
-                    op=ADD,
-                )
-                rounded.append(p_bf)
-            pre_rounded[rnd] = rounded
-
-        def flip_r(rnd):
-            rounded = pre_rounded[rnd]
-            flipped = psum.tile([P, 2, PAIR * P], F32, tag="r_flipped")
-            for s in range(PAIR):
-                words = rounded[s][:].rearrange("r u p v -> r (u p v)").bitcast(F32)
-                for u in range(2):
-                    nc.tensor.transpose(
-                        flipped[:, u, s * P : (s + 1) * P], words[:, u * P : (u + 1) * P], ident_f32[:]
-                    )
-            grouped = work.tile([P, PAIR, P, PACK], BF16, tag="r_grouped", align_bytes=64)
-            nc.scalar.activation(
-                out=grouped[:].rearrange("p s r (u v) -> p (s r) u v", u=2),
-                in_=flipped[:].bitcast(BF16).rearrange("p u (c v) -> p c u v", v=2),
-                func=RELU,
+            nc.vector.tensor_copy(out=mask_f32[:, half, :], in_=mask_bf[:, half, :])
+            nc.vector.tensor_reduce(
+                out=degree[:, half : half + 1],
+                in_=mask_f32[:, half, :],
+                axis=mybir.AxisListType.X,
+                op=ADD,
             )
-            return grouped
-
-        def second_layer(rnd):
-            half, j = half_and_j(rnd)
-            codes, scales = r_quantised[rnd]
-            for s in range(PAIR):
-                cols = slice(s * P, (s + 1) * P)
-                message = psum.tile([P, H], F32, tag="message")
-                mx_pass(message, codes[:, cols], scales[:, cols], W_M2, True, True)
-                mask_j = mask_f32[:, half, j + s : j + s + 1]
-                if s == 0:
-                    nc.vector.scalar_tensor_tensor(
-                        out=running[half][s][:],
-                        in0=message[:],
-                        scalar=mask_j,
-                        in1=running[half][s][:],
-                        op0=MULT,
-                        op1=ADD,
-                    )
-                else:
-                    masked = work.tile([P, H], F32, tag="masked")
-                    nc.scalar.activation(out=masked[:], in_=message[:], func=COPY, scale=mask_j)
-                    nc.gpsimd.tensor_tensor(
-                        out=running[half][s][:], in0=running[half][s][:], in1=masked[:], op=ADD
-                    )
-
-        def start_sums(half):
             even = sums.tile([P, H], F32, tag="even")
             nc.vector.scalar_tensor_tensor(
                 out=even[:],
@@ -292,29 +196,139 @@ def tile_messagepassing_pa_t_kernel(
             nc.gpsimd.memset(odd[:], 0.0)
             running[half] = [even, odd]
 
+        def spread_source_nodes(half, first_j):
+            js = slice(first_j, first_j + SPREAD_CHUNK)
+            codes_of, scales_of = fourfold[half]
+            codes = spread.tile([P, SPREAD_CHUNK, P], U32, tag="spread_codes", align_bytes=64)
+            nc.vector.tensor_copy(
+                out=codes[:].bitcast(I32).rearrange("p j (b i) -> p j b i", b=GRAPHS_PER_HALF),
+                in_=codes_of[:]
+                .bitcast(I32)
+                .rearrange("p (b j f) -> p j b f", b=GRAPHS_PER_HALF, j=NODES)[:, js, :, 0]
+                .unsqueeze(3)
+                .to_broadcast([P, SPREAD_CHUNK, GRAPHS_PER_HALF, NODES]),
+            )
+            scales = spread.tile([P, SPREAD_CHUNK, P], U8, tag="spread_scales", align_bytes=64)
+            nc.vector.tensor_copy(
+                out=scales[:].bitcast(I32).rearrange("p j (b w) -> p j b w", b=GRAPHS_PER_HALF),
+                in_=scales_of[:]
+                .bitcast(I32)
+                .rearrange("p (b j) -> p j b", b=GRAPHS_PER_HALF)[:, js, :]
+                .unsqueeze(3)
+                .to_broadcast([P, SPREAD_CHUNK, GRAPHS_PER_HALF, NODES // 4]),
+            )
+            spread_h[(half, first_j // SPREAD_CHUNK)] = (codes, scales)
+
+        def half_and_j(rnd, pair):
+            half, in_half = divmod(rnd, ROUNDS_PER_HALF)
+            return half, in_half * ROUND_BLOCKS + pair * PAIR
+
+        def first_layer(rnd, pair, e_codes, e_scales):
+            half, j = half_and_j(rnd, pair)
+            h_spread_codes, h_spread_scales = spread_h[(half, j // SPREAD_CHUNK)]
+            rounded = []
+            for s in range(PAIR):
+                cols = slice(s * P, (s + 1) * P)
+                pre = psum.tile([P, H], F32, tag="pre")
+                mx_pass(pre, e_codes[:, cols], e_scales[:, cols], W_E2, True, False)
+                mx_pass(
+                    pre,
+                    h_spread_codes[:, (j + s) % SPREAD_CHUNK, :],
+                    h_spread_scales[:, (j + s) % SPREAD_CHUNK, :],
+                    W_XJ,
+                    False,
+                    True,
+                )
+                p_bf = work.tile([P, 2, P, 2], BF16, tag="p_bf", bufs=2 * ROUND_BLOCKS)
+                nc.vector.tensor_tensor(
+                    out=p_bf[:],
+                    in0=pre[:].rearrange("r (p u v) -> r u p v", u=2, v=2),
+                    in1=target_term[half][:],
+                    op=ADD,
+                )
+                rounded.append(p_bf)
+            return rounded
+
+        def flip_p_pair(rounded):
+            flipped = psum.tile([P, 2, PAIR * P], F32, tag="p_flipped")
+            for s in range(PAIR):
+                words = rounded[s][:].rearrange("r u p v -> r (u p v)").bitcast(F32)
+                for u in range(2):
+                    nc.tensor.transpose(
+                        flipped[:, u, s * P : (s + 1) * P], words[:, u * P : (u + 1) * P], ident[:]
+                    )
+            return flipped
+
+        def relu_and_group(flipped):
+            grouped = work.tile([P, PAIR * P, PACK], BF16, tag="r_grouped", align_bytes=64)
+            nc.scalar.activation(
+                out=grouped[:].rearrange("p c (u v) -> p c u v", u=2),
+                in_=flipped[:].bitcast(BF16).rearrange("p u (c v) -> p c u v", v=2),
+                func=RELU,
+            )
+            return grouped
+
+        def second_layer(rnd, pair, r_codes, r_scales):
+            half, j = half_and_j(rnd, pair)
+            even, odd = running[half]
+            messages = []
+            for s in range(PAIR):
+                cols = slice(s * P, (s + 1) * P)
+                message = psum.tile([P, H], F32, tag="message")
+                mx_pass(message, r_codes[:, cols], r_scales[:, cols], W_M2, True, True)
+                messages.append(message)
+            nc.vector.scalar_tensor_tensor(
+                out=even[:],
+                in0=messages[0][:],
+                scalar=mask_f32[:, half, j : j + 1],
+                in1=even[:],
+                op0=MULT,
+                op1=ADD,
+            )
+            masked = work.tile([P, H], F32, tag="masked")
+            nc.scalar.activation(
+                out=masked[:], in_=messages[1][:], func=COPY, scale=mask_f32[:, half, j + 1 : j + 2]
+            )
+            nc.gpsimd.tensor_tensor(out=odd[:], in0=odd[:], in1=masked[:], op=ADD)
+
         def store_half(half):
             even, odd = running[half]
             nc.vector.tensor_tensor(out=even[:], in0=even[:], in1=odd[:], op=ADD)
             nc.sync.dma_start(out=out_rows[half * P : (half + 1) * P, :], in_=even[:])
 
+        pairs = range(ROUND_PAIRS)
+        e_quantised = {}
+        p_rounded = {}
+        r_quantised = {}
         for now in range(-1, ROUNDS + 2):
             ahead, behind, last = now + 1, now - 1, now - 2
             if ahead < ROUNDS:
-                e_grouped = flip_e(ahead)
+                e_sb = e_of_round[ahead]
+                e_flipped = [
+                    flip_input_pair([e_sb[:, q * PAIR + s, :] for s in range(PAIR)]) for q in pairs
+                ]
             if 0 <= behind < ROUNDS:
-                r_grouped = flip_r(behind)
+                p_flipped = [flip_p_pair(p_rounded[(behind, q)]) for q in pairs]
             if ahead < ROUNDS:
-                e_quantised[ahead] = quantise_pair(e_grouped, "e")
-                half, j = half_and_j(ahead)
-                if j % SPREAD_CHUNK == 0:
-                    spread_h[(half, j // SPREAD_CHUNK)] = spread_source_nodes(half, j)
+                for q in pairs:
+                    e_grouped = work.tile([P, PAIR * P, PACK], BF16, tag="e_grouped", align_bytes=64)
+                    group_words(e_flipped[q], e_grouped)
+                    e_quantised[(ahead, q)] = quantise_pair(e_grouped, "e")
+                half, j = half_and_j(ahead, 0)
                 if j == 0:
-                    start_sums(half)
-            if 0 <= now < ROUNDS:
-                first_layer(now)
-            if 0 <= behind < ROUNDS:
-                r_quantised[behind] = quantise_pair(r_grouped, "r")
-            if 0 <= last < ROUNDS:
-                second_layer(last)
-                if (last + 1) % ROUNDS_PER_HALF == 0:
-                    store_half(last // ROUNDS_PER_HALF)
+                    repeat_h(half)
+                if j % SPREAD_CHUNK == 0:
+                    spread_source_nodes(half, j)
+                if j == 0:
+                    start_half(half)
+            for q in pairs:
+                if 0 <= behind < ROUNDS:
+                    r_grouped = relu_and_group(p_flipped[q])
+                if 0 <= last < ROUNDS:
+                    second_layer(last, q, *r_quantised[(last, q)])
+                if 0 <= now < ROUNDS:
+                    p_rounded[(now, q)] = first_layer(now, q, *e_quantised[(now, q)])
+                if 0 <= behind < ROUNDS:
+                    r_quantised[(behind, q)] = quantise_pair(r_grouped, "r")
+            if 0 <= last < ROUNDS and (last + 1) % ROUNDS_PER_HALF == 0:
+                store_half(last // ROUNDS_PER_HALF)

@@ -22,11 +22,11 @@ PACK = 4
 HALVES = GRAPHS * NODES // P
 GRAPHS_PER_HALF = GRAPHS // HALVES
 PAIR = 2
-ROUND_PAIRS = 2
-ROUND_BLOCKS = ROUND_PAIRS * PAIR
-ROUNDS_PER_HALF = NODES // ROUND_BLOCKS
-ROUNDS = HALVES * ROUNDS_PER_HALF
+PAIRS_PER_HALF = NODES // PAIR
+PAIRS = HALVES * PAIRS_PER_HALF
+E_CHUNK = 4
 SPREAD_CHUNK = 8
+PSUM_BANKS = 8
 W_XI = 0
 W_XJ = 1
 W_E2 = 2
@@ -46,11 +46,11 @@ def tile_messagepassing_pa_t_kernel(
 
     with ExitStack() as ctx:
         keep = ctx.enter_context(tc.tile_pool(name="keep", bufs=1))
-        e_pool = ctx.enter_context(tc.tile_pool(name="e_pool", bufs=ROUNDS))
+        e_pool = ctx.enter_context(tc.tile_pool(name="e_pool", bufs=HALVES * NODES // E_CHUNK))
         spread = ctx.enter_context(tc.tile_pool(name="spread", bufs=2))
-        work = ctx.enter_context(tc.tile_pool(name="work", bufs=2 * ROUND_PAIRS))
+        work = ctx.enter_context(tc.tile_pool(name="work", bufs=3))
         sums = ctx.enter_context(tc.tile_pool(name="sums", bufs=2))
-        psum = ctx.enter_context(tc.psum_pool(name="psum", bufs=2))
+        psum = ctx.enter_context(tc.psum_pool(name="psum", bufs=PSUM_BANKS))
         ctx.enter_context(tc.manual_schedule())
 
         w_planes = keep.tile([P, 4, H], U8, align_bytes=64)
@@ -72,16 +72,15 @@ def tile_messagepassing_pa_t_kernel(
             out=w_words[:, W_XI : W_E2 + 1, :].bitcast(I32),
             in_=w_m1_words.rearrange("g p n t -> p g (n t)").bitcast(I32),
         )
-        e_of_round = []
-        for rnd in range(ROUNDS):
-            half, first_j = divmod(rnd * ROUND_BLOCKS, NODES)
-            e_sb = e_pool.tile([P, ROUND_BLOCKS, H], BF16)
+        e_chunks = []
+        for c in range(HALVES * NODES // E_CHUNK):
+            half, first_j = divmod(c * E_CHUNK, NODES)
+            e_sb = e_pool.tile([P, E_CHUNK, H], BF16)
             nc.sync.dma_start(
-                out=e_sb[:],
-                in_=e_rows[half * P : (half + 1) * P, first_j : first_j + ROUND_BLOCKS, :],
+                out=e_sb[:], in_=e_rows[half * P : (half + 1) * P, first_j : first_j + E_CHUNK, :]
             )
-            e_of_round.append(e_sb)
-            if rnd == 0:
+            e_chunks.append(e_sb)
+            if c == 0:
                 nc.sync.dma_start(
                     out=w_words[:, W_M2, :].bitcast(I32),
                     in_=w_m2_words[0].rearrange("p n t -> p (n t)").bitcast(I32),
@@ -97,7 +96,7 @@ def tile_messagepassing_pa_t_kernel(
         make_identity(nc, ident[:])
 
         def flip_input_pair(sources):
-            flipped = psum.tile([P, 2, PAIR * P], F32, tag="flipped")
+            flipped = psum.tile([P, 2, PAIR * P], F32, tag="bank")
             for s in range(PAIR):
                 words = sources[s].bitcast(F32)
                 for u in range(2):
@@ -165,7 +164,7 @@ def tile_messagepassing_pa_t_kernel(
 
         def start_half(half):
             cols = slice(half * P, (half + 1) * P)
-            a_i = psum.tile([P, H], F32, tag="pre")
+            a_i = psum.tile([P, H], F32, tag="bank")
             mx_pass(a_i, h_codes[:, cols], h_scales[:, cols], W_XI, True, True)
             table = keep.tile([P, 2, P, 2], F32, name="target_term%d" % half)
             nc.vector.tensor_tensor(
@@ -219,17 +218,17 @@ def tile_messagepassing_pa_t_kernel(
             )
             spread_h[(half, first_j // SPREAD_CHUNK)] = (codes, scales)
 
-        def half_and_j(rnd, pair):
-            half, in_half = divmod(rnd, ROUNDS_PER_HALF)
-            return half, in_half * ROUND_BLOCKS + pair * PAIR
+        def half_and_j(pair):
+            half, in_half = divmod(pair, PAIRS_PER_HALF)
+            return half, in_half * PAIR
 
-        def first_layer(rnd, pair, e_codes, e_scales):
-            half, j = half_and_j(rnd, pair)
+        def first_layer(pair, e_codes, e_scales):
+            half, j = half_and_j(pair)
             h_spread_codes, h_spread_scales = spread_h[(half, j // SPREAD_CHUNK)]
             rounded = []
             for s in range(PAIR):
                 cols = slice(s * P, (s + 1) * P)
-                pre = psum.tile([P, H], F32, tag="pre")
+                pre = psum.tile([P, H], F32, tag="bank")
                 mx_pass(pre, e_codes[:, cols], e_scales[:, cols], W_E2, True, False)
                 mx_pass(
                     pre,
@@ -239,7 +238,7 @@ def tile_messagepassing_pa_t_kernel(
                     False,
                     True,
                 )
-                p_bf = work.tile([P, 2, P, 2], BF16, tag="p_bf", bufs=2 * ROUND_BLOCKS)
+                p_bf = work.tile([P, 2, P, 2], BF16, tag="p_bf", bufs=4 * PAIR)
                 nc.vector.tensor_tensor(
                     out=p_bf[:],
                     in0=pre[:].rearrange("r (p u v) -> r u p v", u=2, v=2),
@@ -250,7 +249,7 @@ def tile_messagepassing_pa_t_kernel(
             return rounded
 
         def flip_p_pair(rounded):
-            flipped = psum.tile([P, 2, PAIR * P], F32, tag="p_flipped")
+            flipped = psum.tile([P, 2, PAIR * P], F32, tag="bank")
             for s in range(PAIR):
                 words = rounded[s][:].rearrange("r u p v -> r (u p v)").bitcast(F32)
                 for u in range(2):
@@ -268,13 +267,13 @@ def tile_messagepassing_pa_t_kernel(
             )
             return grouped
 
-        def second_layer(rnd, pair, r_codes, r_scales):
-            half, j = half_and_j(rnd, pair)
+        def second_layer(pair, r_codes, r_scales):
+            half, j = half_and_j(pair)
             even, odd = running[half]
             messages = []
             for s in range(PAIR):
                 cols = slice(s * P, (s + 1) * P)
-                message = psum.tile([P, H], F32, tag="message")
+                message = psum.tile([P, H], F32, tag="bank")
                 mx_pass(message, r_codes[:, cols], r_scales[:, cols], W_M2, True, True)
                 messages.append(message)
             nc.vector.scalar_tensor_tensor(
@@ -296,39 +295,40 @@ def tile_messagepassing_pa_t_kernel(
             nc.vector.tensor_tensor(out=even[:], in0=even[:], in1=odd[:], op=ADD)
             nc.sync.dma_start(out=out_rows[half * P : (half + 1) * P, :], in_=even[:])
 
-        pairs = range(ROUND_PAIRS)
+        def is_pair(pair):
+            return 0 <= pair < PAIRS
+
+        e_grouped = {}
         e_quantised = {}
         p_rounded = {}
+        r_grouped = {}
         r_quantised = {}
-        for now in range(-1, ROUNDS + 2):
-            ahead, behind, last = now + 1, now - 1, now - 2
-            if ahead < ROUNDS:
-                e_sb = e_of_round[ahead]
-                e_flipped = [
-                    flip_input_pair([e_sb[:, q * PAIR + s, :] for s in range(PAIR)]) for q in pairs
-                ]
-            if 0 <= behind < ROUNDS:
-                p_flipped = [flip_p_pair(p_rounded[(behind, q)]) for q in pairs]
-            if ahead < ROUNDS:
-                for q in pairs:
-                    e_grouped = work.tile([P, PAIR * P, PACK], BF16, tag="e_grouped", align_bytes=64)
-                    group_words(e_flipped[q], e_grouped)
-                    e_quantised[(ahead, q)] = quantise_pair(e_grouped, "e")
-                half, j = half_and_j(ahead, 0)
+        for step in range(-2, PAIRS + 5):
+            if is_pair(step + 2):
+                half, j = half_and_j(step + 2)
+                e_sb = e_chunks[(half * NODES + j) // E_CHUNK]
+                e_flipped = flip_input_pair([e_sb[:, (j + s) % E_CHUNK, :] for s in range(PAIR)])
+            if is_pair(step - 2):
+                p_flipped = flip_p_pair(p_rounded[step - 2])
+            if is_pair(step - 3):
+                r_quantised[step - 3] = quantise_pair(r_grouped[step - 3], "r")
+            if is_pair(step + 1):
+                e_quantised[step + 1] = quantise_pair(e_grouped[step + 1], "e")
+            if is_pair(step + 2):
+                grouped = work.tile([P, PAIR * P, PACK], BF16, tag="e_grouped", align_bytes=64)
+                group_words(e_flipped, grouped)
+                e_grouped[step + 2] = grouped
                 if j == 0:
                     repeat_h(half)
                 if j % SPREAD_CHUNK == 0:
                     spread_source_nodes(half, j)
                 if j == 0:
                     start_half(half)
-            for q in pairs:
-                if 0 <= behind < ROUNDS:
-                    r_grouped = relu_and_group(p_flipped[q])
-                if 0 <= last < ROUNDS:
-                    second_layer(last, q, *r_quantised[(last, q)])
-                if 0 <= now < ROUNDS:
-                    p_rounded[(now, q)] = first_layer(now, q, *e_quantised[(now, q)])
-                if 0 <= behind < ROUNDS:
-                    r_quantised[(behind, q)] = quantise_pair(r_grouped, "r")
-            if 0 <= last < ROUNDS and (last + 1) % ROUNDS_PER_HALF == 0:
-                store_half(last // ROUNDS_PER_HALF)
+            if is_pair(step - 2):
+                r_grouped[step - 2] = relu_and_group(p_flipped)
+            if is_pair(step - 4):
+                second_layer(step - 4, *r_quantised[step - 4])
+                if (step - 4 + 1) % PAIRS_PER_HALF == 0:
+                    store_half((step - 4) // PAIRS_PER_HALF)
+            if is_pair(step):
+                p_rounded[step] = first_layer(step, *e_quantised[step])

@@ -27,6 +27,7 @@ PAIRS = HALVES * PAIRS_PER_HALF
 E_CHUNK = 4
 SPREAD_CHUNK = 8
 PSUM_BANKS = 8
+E_LEAD = 4
 W_XI = 0
 W_XJ = 1
 W_E2 = 2
@@ -55,23 +56,17 @@ def tile_messagepassing_pa_t_kernel(
 
         w_planes = keep.tile([P, 4, H], U8, align_bytes=64)
         nc.vector.memset(w_planes[:].bitcast(I32), 0)
+        w_words = keep.tile([P, 4, H], U32, align_bytes=64)
         h_sb = keep.tile([P, HALVES, H], BF16)
         nc.sync.dma_start(out=h_sb[:], in_=h_rows.rearrange("(s p) k -> p s k", p=P))
-        for quad in range(4):
-            live = slice(32 * quad, 32 * quad + 4)
-            rows = slice(4 * quad, 4 * quad + 4)
-            nc.sync.dma_start(
-                out=w_planes[live, W_XI : W_E2 + 1, :].bitcast(I32),
-                in_=w_m1_scales[:, rows, :].bitcast(I32).rearrange("g r n -> r g n"),
-            )
-            nc.sync.dma_start(
-                out=w_planes[live, W_M2, :].bitcast(I32), in_=w_m2_scales[0, rows, :].bitcast(I32)
-            )
-        w_words = keep.tile([P, 4, H], U32, align_bytes=64)
-        nc.sync.dma_start(
-            out=w_words[:, W_XI : W_E2 + 1, :].bitcast(I32),
-            in_=w_m1_words.rearrange("g p n t -> p g (n t)").bitcast(I32),
-        )
+
+        def load_scale_rows(planes, scale_rows):
+            for quad in range(4):
+                nc.sync.dma_start(
+                    out=planes[32 * quad : 32 * quad + 4].bitcast(I32),
+                    in_=scale_rows[4 * quad : 4 * quad + 4].bitcast(I32),
+                )
+
         e_chunks = []
         for c in range(HALVES * NODES // E_CHUNK):
             half, first_j = divmod(c * E_CHUNK, NODES)
@@ -82,9 +77,18 @@ def tile_messagepassing_pa_t_kernel(
             e_chunks.append(e_sb)
             if c == 0:
                 nc.sync.dma_start(
+                    out=w_words[:, W_XI : W_E2 + 1, :].bitcast(I32),
+                    in_=w_m1_words.rearrange("g p n t -> p g (n t)").bitcast(I32),
+                )
+                load_scale_rows(
+                    w_planes[:, W_XI : W_E2 + 1, :], w_m1_scales.rearrange("g r n -> r g n")
+                )
+            if c == 1:
+                nc.sync.dma_start(
                     out=w_words[:, W_M2, :].bitcast(I32),
                     in_=w_m2_words[0].rearrange("p n t -> p (n t)").bitcast(I32),
                 )
+                load_scale_rows(w_planes[:, W_M2, :], w_m2_scales[0])
         b1_all = keep.tile([P, H], BF16)
         nc.scalar.dma_start(out=b1_all[:], in_=b_m1.partition_broadcast(P))
         mask_bf = keep.tile([P, HALVES, NODES], BF16)
@@ -116,8 +120,8 @@ def tile_messagepassing_pa_t_kernel(
             )
 
         def quantise_pair(grouped, tag):
-            codes = work.tile([P, PAIR * P], U32, tag=tag + "_codes", align_bytes=64)
-            scales = work.tile([P, PAIR * P], U8, tag=tag + "_scales", align_bytes=64)
+            codes = work.tile([P, PAIR * P], U32, tag=tag + "_codes", bufs=E_LEAD + 1, align_bytes=64)
+            scales = work.tile([P, PAIR * P], U8, tag=tag + "_scales", bufs=E_LEAD + 1, align_bytes=64)
             quantise(grouped, codes, scales)
             return codes, scales
 
@@ -182,18 +186,18 @@ def tile_messagepassing_pa_t_kernel(
                 axis=mybir.AxisListType.X,
                 op=ADD,
             )
-            even = sums.tile([P, H], F32, tag="even")
+            by_vector = sums.tile([P, H], F32, tag="by_vector")
             nc.vector.scalar_tensor_tensor(
-                out=even[:],
+                out=by_vector[:],
                 in0=b2_all[:],
                 scalar=degree[:, half : half + 1],
                 in1=h_sb[:, half, :],
                 op0=MULT,
                 op1=ADD,
             )
-            odd = sums.tile([P, H], F32, tag="odd")
-            nc.gpsimd.memset(odd[:], 0.0)
-            running[half] = [even, odd]
+            by_gpsimd = sums.tile([P, H], F32, tag="by_gpsimd")
+            nc.gpsimd.memset(by_gpsimd[:], 0.0)
+            running[half] = [by_vector, by_gpsimd]
 
         def spread_source_nodes(half, first_j):
             js = slice(first_j, first_j + SPREAD_CHUNK)
@@ -267,33 +271,40 @@ def tile_messagepassing_pa_t_kernel(
             )
             return grouped
 
-        def second_layer(pair, r_codes, r_scales):
-            half, j = half_and_j(pair)
-            even, odd = running[half]
+        def second_layer_passes(pair, r_codes, r_scales):
             messages = []
             for s in range(PAIR):
                 cols = slice(s * P, (s + 1) * P)
                 message = psum.tile([P, H], F32, tag="bank")
                 mx_pass(message, r_codes[:, cols], r_scales[:, cols], W_M2, True, True)
                 messages.append(message)
+            return messages
+
+        def mask_and_add_on_vector(message, half, j):
+            by_vector = running[half][0]
             nc.vector.scalar_tensor_tensor(
-                out=even[:],
-                in0=messages[0][:],
+                out=by_vector[:],
+                in0=message[:],
                 scalar=mask_f32[:, half, j : j + 1],
-                in1=even[:],
+                in1=by_vector[:],
                 op0=MULT,
                 op1=ADD,
             )
+
+        def mask_on_scalar_add_on_gpsimd(message, half, j):
+            by_gpsimd = running[half][1]
             masked = work.tile([P, H], F32, tag="masked")
             nc.scalar.activation(
-                out=masked[:], in_=messages[1][:], func=COPY, scale=mask_f32[:, half, j + 1 : j + 2]
+                out=masked[:], in_=message[:], func=COPY, scale=mask_f32[:, half, j : j + 1]
             )
-            nc.gpsimd.tensor_tensor(out=odd[:], in0=odd[:], in1=masked[:], op=ADD)
+            nc.gpsimd.tensor_tensor(out=by_gpsimd[:], in0=by_gpsimd[:], in1=masked[:], op=ADD)
+
+        def join_sums(half):
+            by_vector, by_gpsimd = running[half]
+            nc.vector.tensor_tensor(out=by_vector[:], in0=by_vector[:], in1=by_gpsimd[:], op=ADD)
 
         def store_half(half):
-            even, odd = running[half]
-            nc.vector.tensor_tensor(out=even[:], in0=even[:], in1=odd[:], op=ADD)
-            nc.sync.dma_start(out=out_rows[half * P : (half + 1) * P, :], in_=even[:])
+            nc.sync.dma_start(out=out_rows[half * P : (half + 1) * P, :], in_=running[half][0][:])
 
         def is_pair(pair):
             return 0 <= pair < PAIRS
@@ -303,32 +314,44 @@ def tile_messagepassing_pa_t_kernel(
         p_rounded = {}
         r_grouped = {}
         r_quantised = {}
-        for step in range(-2, PAIRS + 5):
-            if is_pair(step + 2):
-                half, j = half_and_j(step + 2)
+        repeat_h(0)
+        spread_source_nodes(0, 0)
+        for step in range(-E_LEAD, PAIRS + 5):
+            if is_pair(step + E_LEAD):
+                half, j = half_and_j(step + E_LEAD)
                 e_sb = e_chunks[(half * NODES + j) // E_CHUNK]
                 e_flipped = flip_input_pair([e_sb[:, (j + s) % E_CHUNK, :] for s in range(PAIR)])
             if is_pair(step - 2):
                 p_flipped = flip_p_pair(p_rounded[step - 2])
             if is_pair(step - 3):
                 r_quantised[step - 3] = quantise_pair(r_grouped[step - 3], "r")
-            if is_pair(step + 1):
-                e_quantised[step + 1] = quantise_pair(e_grouped[step + 1], "e")
-            if is_pair(step + 2):
+            if is_pair(step + E_LEAD - 1):
+                e_quantised[step + E_LEAD - 1] = quantise_pair(e_grouped[step + E_LEAD - 1], "e")
+            if is_pair(step + E_LEAD):
                 grouped = work.tile([P, PAIR * P, PACK], BF16, tag="e_grouped", align_bytes=64)
                 group_words(e_flipped, grouped)
-                e_grouped[step + 2] = grouped
+                e_grouped[step + E_LEAD] = grouped
+            if 0 < step + 2 < PAIRS:
+                half, j = half_and_j(step + 2)
                 if j == 0:
                     repeat_h(half)
                 if j % SPREAD_CHUNK == 0:
                     spread_source_nodes(half, j)
-                if j == 0:
-                    start_half(half)
+            if is_pair(step - 4):
+                half, j = half_and_j(step - 4)
+                messages = second_layer_passes(step - 4, *r_quantised[step - 4])
+                if j + PAIR < NODES:
+                    mask_on_scalar_add_on_gpsimd(messages[0], half, j)
+                    mask_and_add_on_vector(messages[1], half, j + 1)
+                else:
+                    join_sums(half)
+                    mask_and_add_on_vector(messages[0], half, j)
+                    mask_and_add_on_vector(messages[1], half, j + 1)
+                    store_half(half)
             if is_pair(step - 2):
                 r_grouped[step - 2] = relu_and_group(p_flipped)
-            if is_pair(step - 4):
-                second_layer(step - 4, *r_quantised[step - 4])
-                if (step - 4 + 1) % PAIRS_PER_HALF == 0:
-                    store_half((step - 4) // PAIRS_PER_HALF)
             if is_pair(step):
+                half, j = half_and_j(step)
+                if j == 0:
+                    start_half(half)
                 p_rounded[step] = first_layer(step, *e_quantised[step])

@@ -52,7 +52,6 @@ def tile_messagepassing_pa_t_kernel(
         work = ctx.enter_context(tc.tile_pool(name="work", bufs=3))
         sums = ctx.enter_context(tc.tile_pool(name="sums", bufs=2))
         psum = ctx.enter_context(tc.psum_pool(name="psum", bufs=PSUM_BANKS))
-        ctx.enter_context(tc.manual_schedule())
 
         w_planes = keep.tile([P, 4, H], U8, align_bytes=64)
         nc.vector.memset(w_planes[:].bitcast(I32), 0)

@@ -52,6 +52,7 @@ def tile_messagepassing_pa_t_kernel(
         work = ctx.enter_context(tc.tile_pool(name="work", bufs=3))
         sums = ctx.enter_context(tc.tile_pool(name="sums", bufs=2))
         psum = ctx.enter_context(tc.psum_pool(name="psum", bufs=PSUM_BANKS))
+        ctx.enter_context(tc.manual_schedule())
 
         w_planes = keep.tile([P, 4, H], U8, align_bytes=64)
         nc.vector.memset(w_planes[:].bitcast(I32), 0)
@@ -109,20 +110,10 @@ def tile_messagepassing_pa_t_kernel(
             return flipped
 
         def group_words(flipped, grouped):
-            nc.scalar.copy(out=grouped[:].bitcast(F32), in_=flipped[:].rearrange("p u c -> p c u"))
+            nc.scalar.copy(out=grouped.bitcast(F32), in_=flipped[:].rearrange("p u c -> p c u"))
 
         def quantise(grouped, codes, scales):
-            nc.vector.quantize_mx(
-                out=codes[:].bitcast(FP8X4),
-                scales=scales[:],
-                in_=grouped[:].rearrange("p c t -> p (c t)"),
-            )
-
-        def quantise_pair(grouped, tag):
-            codes = work.tile([P, PAIR * P], U32, tag=tag + "_codes", bufs=E_LEAD + 1, align_bytes=64)
-            scales = work.tile([P, PAIR * P], U8, tag=tag + "_scales", bufs=E_LEAD + 1, align_bytes=64)
-            quantise(grouped, codes, scales)
-            return codes, scales
+            nc.vector.quantize_mx(out=codes.bitcast(FP8X4), scales=scales, in_=grouped)
 
         def mx_pass(acc, codes, scales, weight, start, stop):
             nc.tensor.matmul_mx(
@@ -136,10 +127,10 @@ def tile_messagepassing_pa_t_kernel(
             )
 
         h_grouped = keep.tile([P, HALVES * P, PACK], BF16, align_bytes=64)
-        group_words(flip_input_pair([h_sb[:, 0, :], h_sb[:, 1, :]]), h_grouped)
+        group_words(flip_input_pair([h_sb[:, 0, :], h_sb[:, 1, :]]), h_grouped[:])
         h_codes = keep.tile([P, HALVES * P], U32, align_bytes=64)
         h_scales = keep.tile([P, HALVES * P], U8, align_bytes=64)
-        quantise(h_grouped, h_codes, h_scales)
+        quantise(h_grouped[:].rearrange("p c t -> p (c t)"), h_codes[:], h_scales[:])
         mask_f32 = keep.tile([P, HALVES, NODES], F32)
         degree = keep.tile([P, HALVES], F32)
 
@@ -261,14 +252,12 @@ def tile_messagepassing_pa_t_kernel(
                     )
             return flipped
 
-        def relu_and_group(flipped):
-            grouped = work.tile([P, PAIR * P, PACK], BF16, tag="r_grouped", align_bytes=64)
+        def relu_and_group(flipped, grouped):
             nc.scalar.activation(
-                out=grouped[:].rearrange("p c (u v) -> p c u v", u=2),
+                out=grouped.rearrange("p c (u v) -> p c u v", u=2),
                 in_=flipped[:].bitcast(BF16).rearrange("p u (c v) -> p c u v", v=2),
                 func=RELU,
             )
-            return grouped
 
         def second_layer_passes(pair, r_codes, r_scales):
             messages = []
@@ -305,14 +294,15 @@ def tile_messagepassing_pa_t_kernel(
         def store_half(half):
             nc.sync.dma_start(out=out_rows[half * P : (half + 1) * P, :], in_=running[half][0][:])
 
+        E_PART = 0
+        R_PART = 1
+
         def is_pair(pair):
             return 0 <= pair < PAIRS
 
-        e_grouped = {}
-        e_quantised = {}
+        grouped_in = {}
+        quantised_in = {}
         p_rounded = {}
-        r_grouped = {}
-        r_quantised = {}
         repeat_h(0)
         spread_source_nodes(0, 0)
         for step in range(-E_LEAD, PAIRS + 5):
@@ -322,14 +312,24 @@ def tile_messagepassing_pa_t_kernel(
                 e_flipped = flip_input_pair([e_sb[:, (j + s) % E_CHUNK, :] for s in range(PAIR)])
             if is_pair(step - 2):
                 p_flipped = flip_p_pair(p_rounded[step - 2])
-            if is_pair(step - 3):
-                r_quantised[step - 3] = quantise_pair(r_grouped[step - 3], "r")
-            if is_pair(step + E_LEAD - 1):
-                e_quantised[step + E_LEAD - 1] = quantise_pair(e_grouped[step + E_LEAD - 1], "e")
+            if step - 1 in grouped_in:
+                parts = slice(
+                    E_PART if is_pair(step - 1 + E_LEAD) else R_PART,
+                    R_PART + 1 if is_pair(step - 1 - 2) else R_PART,
+                )
+                codes = work.tile([P, 2, PAIR * P], U32, tag="codes", bufs=E_LEAD + 1, align_bytes=64)
+                scales = work.tile([P, 2, PAIR * P], U8, tag="scales", bufs=E_LEAD + 1, align_bytes=64)
+                quantise(
+                    grouped_in[step - 1][:, parts].rearrange("p k c t -> p (k c t)"),
+                    codes[:, parts, :].rearrange("p k c -> p (k c)"),
+                    scales[:, parts, :].rearrange("p k c -> p (k c)"),
+                )
+                quantised_in[step - 1] = (codes, scales)
+            if is_pair(step + E_LEAD) or is_pair(step - 2):
+                grouped = work.tile([P, 2, PAIR * P, PACK], BF16, tag="grouped", align_bytes=64)
+                grouped_in[step] = grouped
             if is_pair(step + E_LEAD):
-                grouped = work.tile([P, PAIR * P, PACK], BF16, tag="e_grouped", align_bytes=64)
-                group_words(e_flipped, grouped)
-                e_grouped[step + E_LEAD] = grouped
+                group_words(e_flipped, grouped[:, E_PART])
             if 0 < step + 2 < PAIRS:
                 half, j = half_and_j(step + 2)
                 if j == 0:
@@ -338,7 +338,8 @@ def tile_messagepassing_pa_t_kernel(
                     spread_source_nodes(half, j)
             if is_pair(step - 4):
                 half, j = half_and_j(step - 4)
-                messages = second_layer_passes(step - 4, *r_quantised[step - 4])
+                codes, scales = quantised_in[step - 2]
+                messages = second_layer_passes(step - 4, codes[:, R_PART, :], scales[:, R_PART, :])
                 if j + PAIR < NODES:
                     mask_on_scalar_add_on_gpsimd(messages[0], half, j)
                     mask_and_add_on_vector(messages[1], half, j + 1)
@@ -348,9 +349,10 @@ def tile_messagepassing_pa_t_kernel(
                     mask_and_add_on_vector(messages[1], half, j + 1)
                     store_half(half)
             if is_pair(step - 2):
-                r_grouped[step - 2] = relu_and_group(p_flipped)
+                relu_and_group(p_flipped, grouped[:, R_PART])
             if is_pair(step):
                 half, j = half_and_j(step)
                 if j == 0:
                     start_half(half)
-                p_rounded[step] = first_layer(step, *e_quantised[step])
+                codes, scales = quantised_in[step - E_LEAD]
+                p_rounded[step] = first_layer(step, codes[:, E_PART, :], scales[:, E_PART, :])

@@ -11,6 +11,7 @@ U8 = mybir.dt.uint8
 FP8X4 = mybir.dt.float8_e4m3fn_x4
 ADD = mybir.AluOpType.add
 MULT = mybir.AluOpType.mult
+MAX = mybir.AluOpType.max
 RELU = mybir.ActivationFunctionType.Relu
 COPY = mybir.ActivationFunctionType.Copy
 
@@ -25,9 +26,8 @@ PAIR = 2
 PAIRS_PER_HALF = NODES // PAIR
 PAIRS = HALVES * PAIRS_PER_HALF
 E_CHUNK = 4
-SPREAD_CHUNK = 8
 PSUM_BANKS = 8
-E_LEAD = 4
+E_LEAD = 3
 W_XI = 0
 W_XJ = 1
 W_E2 = 2
@@ -47,8 +47,7 @@ def tile_messagepassing_pa_t_kernel(
 
     with ExitStack() as ctx:
         keep = ctx.enter_context(tc.tile_pool(name="keep", bufs=1))
-        e_pool = ctx.enter_context(tc.tile_pool(name="e_pool", bufs=HALVES * NODES // E_CHUNK))
-        spread = ctx.enter_context(tc.tile_pool(name="spread", bufs=2))
+        e_pool = ctx.enter_context(tc.tile_pool(name="e_pool", bufs=HALVES * NODES // E_CHUNK + 1))
         work = ctx.enter_context(tc.tile_pool(name="work", bufs=3))
         sums = ctx.enter_context(tc.tile_pool(name="sums", bufs=2))
         psum = ctx.enter_context(tc.psum_pool(name="psum", bufs=PSUM_BANKS))
@@ -67,30 +66,37 @@ def tile_messagepassing_pa_t_kernel(
                     in_=scale_rows[4 * quad : 4 * quad + 4].bitcast(I32),
                 )
 
-        e_chunks = []
-        for c in range(HALVES * NODES // E_CHUNK):
-            half, first_j = divmod(c * E_CHUNK, NODES)
-            e_sb = e_pool.tile([P, E_CHUNK, H], BF16)
+        def load_w_m1(weight):
             nc.sync.dma_start(
-                out=e_sb[:], in_=e_rows[half * P : (half + 1) * P, first_j : first_j + E_CHUNK, :]
+                out=w_words[:, weight, :].bitcast(I32),
+                in_=w_m1_words[weight].rearrange("p n t -> p (n t)").bitcast(I32),
             )
-            e_chunks.append(e_sb)
-            if c == 0:
-                nc.sync.dma_start(
-                    out=w_words[:, W_XI : W_E2 + 1, :].bitcast(I32),
-                    in_=w_m1_words.rearrange("g p n t -> p g (n t)").bitcast(I32),
-                )
-                load_scale_rows(
-                    w_planes[:, W_XI : W_E2 + 1, :], w_m1_scales.rearrange("g r n -> r g n")
-                )
-            if c == 1:
-                nc.sync.dma_start(
-                    out=w_words[:, W_M2, :].bitcast(I32),
-                    in_=w_m2_words[0].rearrange("p n t -> p (n t)").bitcast(I32),
-                )
-                load_scale_rows(w_planes[:, W_M2, :], w_m2_scales[0])
-        b1_all = keep.tile([P, H], BF16)
-        nc.scalar.dma_start(out=b1_all[:], in_=b_m1.partition_broadcast(P))
+
+        e_blocks = []
+
+        def load_e(blocks):
+            half, j = divmod(len(e_blocks), NODES)
+            e_sb = e_pool.tile([P, blocks, H], BF16)
+            nc.sync.dma_start(
+                out=e_sb[:], in_=e_rows[half * P : (half + 1) * P, j : j + blocks, :]
+            )
+            e_blocks.extend([e_sb[:, s, :] for s in range(blocks)])
+
+        load_w_m1(W_XJ)
+        load_scale_rows(w_planes[:, W_XI : W_E2 + 1, :], w_m1_scales.rearrange("g r n -> r g n"))
+        load_e(PAIR)
+        load_w_m1(W_E2)
+        load_w_m1(W_XI)
+        load_e(PAIR)
+        nc.sync.dma_start(
+            out=w_words[:, W_M2, :].bitcast(I32),
+            in_=w_m2_words[0].rearrange("p n t -> p (n t)").bitcast(I32),
+        )
+        load_scale_rows(w_planes[:, W_M2, :], w_m2_scales[0])
+        while len(e_blocks) < HALVES * NODES:
+            load_e(E_CHUNK)
+        b1 = keep.tile([P, PACK], BF16)
+        nc.scalar.dma_start(out=b1[:], in_=b_m1.rearrange("(p t) -> p t", t=PACK))
         mask_bf = keep.tile([P, HALVES, NODES], BF16)
         nc.scalar.dma_start(out=mask_bf[:], in_=mask_rows.rearrange("(s p) j -> p s j", p=P))
         b2_all = keep.tile([P, H], BF16)
@@ -115,16 +121,33 @@ def tile_messagepassing_pa_t_kernel(
         def quantise(grouped, codes, scales):
             nc.vector.quantize_mx(out=codes.bitcast(FP8X4), scales=scales, in_=grouped)
 
-        def mx_pass(acc, codes, scales, weight, start, stop):
+        def mx_pass(acc, left, right, start, stop):
             nc.tensor.matmul_mx(
-                out=acc[:],
-                lhsT=codes.bitcast(FP8X4),
-                lhsT_scale=scales,
-                rhs=w_words[:, weight, :].bitcast(FP8X4),
-                rhs_scale=w_planes[:, weight, :],
+                out=acc,
+                lhsT=left[0].bitcast(FP8X4),
+                lhsT_scale=left[1],
+                rhs=right[0].bitcast(FP8X4),
+                rhs_scale=right[1],
                 start=start,
                 stop=stop,
             )
+
+        t_words = keep.tile([P, 3, H], U32, align_bytes=64)
+        t_planes = keep.tile([P, 3, H], U8, align_bytes=64)
+
+        def order_columns(weight):
+            nc.vector.tensor_copy(
+                out=t_words[:, weight, :].bitcast(I32).rearrange("p (t m) -> p m t", t=PACK),
+                in_=w_words[:, weight, :].bitcast(I32).rearrange("p (m t) -> p m t", t=PACK),
+            )
+            nc.vector.tensor_copy(
+                out=t_planes[:, weight, :].rearrange("p (t m) -> p m t", t=PACK),
+                in_=w_planes[:, weight, :].rearrange("p (m t) -> p m t", t=PACK),
+            )
+
+        def channels(weight, t):
+            cols = slice(t * P, (t + 1) * P)
+            return t_words[:, weight, cols], t_planes[:, weight, cols]
 
         h_grouped = keep.tile([P, HALVES * P, PACK], BF16, align_bytes=64)
         group_words(flip_input_pair([h_sb[:, 0, :], h_sb[:, 1, :]]), h_grouped[:])
@@ -134,41 +157,27 @@ def tile_messagepassing_pa_t_kernel(
         mask_f32 = keep.tile([P, HALVES, NODES], F32)
         degree = keep.tile([P, HALVES], F32)
 
-        target_term = {}
-        fourfold = {}
+        source_term = {}
         running = {}
-        spread_h = {}
 
-        def repeat_h(half):
+        def nodes_of(half):
             cols = slice(half * P, (half + 1) * P)
-            repeated = keep.tile([P, P, 4, PACK], BF16, name="repeated%d" % half, align_bytes=64)
-            nc.scalar.copy(
-                out=repeated[:].bitcast(F32),
-                in_=h_grouped[:, cols, :].bitcast(F32).unsqueeze(2).to_broadcast([P, P, 4, 2]),
-            )
-            codes = keep.tile([P, P * 4], U32, name="fourfold_codes%d" % half, align_bytes=64)
-            scales = keep.tile([P, P * 4], U8, name="fourfold_scales%d" % half, align_bytes=64)
-            nc.vector.memset(scales[:].bitcast(I32), 0)
-            nc.vector.quantize_mx(
-                out=codes[:].bitcast(FP8X4),
-                scales=scales[:],
-                in_=repeated[:].rearrange("p c f t -> p (c f t)"),
-            )
-            fourfold[half] = (codes, scales)
+            return h_codes[:, cols], h_scales[:, cols]
 
-        def start_half(half):
-            cols = slice(half * P, (half + 1) * P)
-            a_i = psum.tile([P, H], F32, tag="bank")
-            mx_pass(a_i, h_codes[:, cols], h_scales[:, cols], W_XI, True, True)
-            table = keep.tile([P, 2, P, 2], F32, name="target_term%d" % half)
+        def make_source_term(half):
+            a_j = psum.tile([P, PACK, P], F32, tag="bank")
+            for t in range(PACK):
+                mx_pass(a_j[:, t, :], channels(W_XJ, t), nodes_of(half), True, True)
+            table = keep.tile([P, P, PACK], F32, name="source_term%d" % half)
             nc.vector.tensor_tensor(
                 out=table[:],
-                in0=a_i[:].rearrange("r (p u v) -> r u p v", u=2, v=2),
-                in1=b1_all[:].rearrange("r (p u v) -> r u p v", u=2, v=2),
+                in0=a_j[:].rearrange("p t c -> p c t"),
+                in1=b1[:].unsqueeze(1).to_broadcast([P, P, PACK]),
                 op=ADD,
             )
-            target_term[half] = table
+            source_term[half] = table
 
+        def start_sums(half):
             nc.vector.tensor_copy(out=mask_f32[:, half, :], in_=mask_bf[:, half, :])
             nc.vector.tensor_reduce(
                 out=degree[:, half : half + 1],
@@ -189,82 +198,56 @@ def tile_messagepassing_pa_t_kernel(
             nc.gpsimd.memset(by_gpsimd[:], 0.0)
             running[half] = [by_vector, by_gpsimd]
 
-        def spread_source_nodes(half, first_j):
-            js = slice(first_j, first_j + SPREAD_CHUNK)
-            codes_of, scales_of = fourfold[half]
-            codes = spread.tile([P, SPREAD_CHUNK, P], U32, tag="spread_codes", align_bytes=64)
-            nc.vector.tensor_copy(
-                out=codes[:].bitcast(I32).rearrange("p j (b i) -> p j b i", b=GRAPHS_PER_HALF),
-                in_=codes_of[:]
-                .bitcast(I32)
-                .rearrange("p (b j f) -> p j b f", b=GRAPHS_PER_HALF, j=NODES)[:, js, :, 0]
-                .unsqueeze(3)
-                .to_broadcast([P, SPREAD_CHUNK, GRAPHS_PER_HALF, NODES]),
-            )
-            scales = spread.tile([P, SPREAD_CHUNK, P], U8, tag="spread_scales", align_bytes=64)
-            nc.vector.tensor_copy(
-                out=scales[:].bitcast(I32).rearrange("p j (b w) -> p j b w", b=GRAPHS_PER_HALF),
-                in_=scales_of[:]
-                .bitcast(I32)
-                .rearrange("p (b j) -> p j b", b=GRAPHS_PER_HALF)[:, js, :]
-                .unsqueeze(3)
-                .to_broadcast([P, SPREAD_CHUNK, GRAPHS_PER_HALF, NODES // 4]),
-            )
-            spread_h[(half, first_j // SPREAD_CHUNK)] = (codes, scales)
-
         def half_and_j(pair):
             half, in_half = divmod(pair, PAIRS_PER_HALF)
             return half, in_half * PAIR
 
         def first_layer(pair, e_codes, e_scales):
             half, j = half_and_j(pair)
-            h_spread_codes, h_spread_scales = spread_h[(half, j // SPREAD_CHUNK)]
-            rounded = []
+            p_bf = work.tile([P, PAIR, P, PACK], BF16, tag="p_bf")
             for s in range(PAIR):
                 cols = slice(s * P, (s + 1) * P)
-                pre = psum.tile([P, H], F32, tag="bank")
-                mx_pass(pre, e_codes[:, cols], e_scales[:, cols], W_E2, True, False)
-                mx_pass(
-                    pre,
-                    h_spread_codes[:, (j + s) % SPREAD_CHUNK, :],
-                    h_spread_scales[:, (j + s) % SPREAD_CHUNK, :],
-                    W_XJ,
-                    False,
-                    True,
-                )
-                p_bf = work.tile([P, 2, P, 2], BF16, tag="p_bf", bufs=4 * PAIR)
+                pre = psum.tile([P, PACK, P], F32, tag="bank")
+                for t in range(PACK):
+                    mx_pass(
+                        pre[:, t, :],
+                        channels(W_E2, t),
+                        (e_codes[:, cols], e_scales[:, cols]),
+                        True,
+                        False,
+                    )
+                    mx_pass(pre[:, t, :], channels(W_XI, t), nodes_of(half), False, True)
                 nc.vector.tensor_tensor(
-                    out=p_bf[:],
-                    in0=pre[:].rearrange("r (p u v) -> r u p v", u=2, v=2),
-                    in1=target_term[half][:],
+                    out=p_bf[:, s].rearrange("p (b i) t -> p b i t", b=GRAPHS_PER_HALF),
+                    in0=pre[:].rearrange("p t (b i) -> p b i t", b=GRAPHS_PER_HALF),
+                    in1=source_term[half][:]
+                    .rearrange("p (b j) t -> p b j t", b=GRAPHS_PER_HALF)[:, :, j + s, :]
+                    .unsqueeze(2)
+                    .to_broadcast([P, GRAPHS_PER_HALF, NODES, PACK]),
                     op=ADD,
                 )
-                rounded.append(p_bf)
-            return rounded
+            return p_bf
 
-        def flip_p_pair(rounded):
-            flipped = psum.tile([P, 2, PAIR * P], F32, tag="bank")
-            for s in range(PAIR):
-                words = rounded[s][:].rearrange("r u p v -> r (u p v)").bitcast(F32)
-                for u in range(2):
-                    nc.tensor.transpose(
-                        flipped[:, u, s * P : (s + 1) * P], words[:, u * P : (u + 1) * P], ident[:]
-                    )
-            return flipped
-
-        def relu_and_group(flipped, grouped):
-            nc.scalar.activation(
-                out=grouped.rearrange("p c (u v) -> p c u v", u=2),
-                in_=flipped[:].bitcast(BF16).rearrange("p u (c v) -> p c u v", v=2),
-                func=RELU,
-            )
+        def relu(pair, grouped):
+            p_bf = p_rounded[pair][:].rearrange("p s c t -> p (s c t)")
+            r = grouped.rearrange("p c t -> p (c t)")
+            if pair < PAIRS - 1:
+                nc.scalar.activation(out=r, in_=p_bf, func=RELU)
+            else:
+                nc.vector.tensor_scalar(out=r, in0=p_bf, scalar1=0.0, scalar2=None, op0=MAX)
 
         def second_layer_passes(pair, r_codes, r_scales):
             messages = []
             for s in range(PAIR):
                 cols = slice(s * P, (s + 1) * P)
                 message = psum.tile([P, H], F32, tag="bank")
-                mx_pass(message, r_codes[:, cols], r_scales[:, cols], W_M2, True, True)
+                mx_pass(
+                    message[:],
+                    (r_codes[:, cols], r_scales[:, cols]),
+                    (w_words[:, W_M2, :], w_planes[:, W_M2, :]),
+                    True,
+                    True,
+                )
                 messages.append(message)
             return messages
 
@@ -303,19 +286,18 @@ def tile_messagepassing_pa_t_kernel(
         grouped_in = {}
         quantised_in = {}
         p_rounded = {}
-        repeat_h(0)
-        spread_source_nodes(0, 0)
-        for step in range(-E_LEAD, PAIRS + 5):
+        order_columns(W_XJ)
+        make_source_term(0)
+        order_columns(W_E2)
+        order_columns(W_XI)
+        for step in range(-E_LEAD, PAIRS + 4):
             if is_pair(step + E_LEAD):
-                half, j = half_and_j(step + E_LEAD)
-                e_sb = e_chunks[(half * NODES + j) // E_CHUNK]
-                e_flipped = flip_input_pair([e_sb[:, (j + s) % E_CHUNK, :] for s in range(PAIR)])
-            if is_pair(step - 2):
-                p_flipped = flip_p_pair(p_rounded[step - 2])
+                first = (step + E_LEAD) * PAIR
+                e_flipped = flip_input_pair(e_blocks[first : first + PAIR])
             if step - 1 in grouped_in:
                 parts = slice(
                     E_PART if is_pair(step - 1 + E_LEAD) else R_PART,
-                    R_PART + 1 if is_pair(step - 1 - 2) else R_PART,
+                    R_PART + 1 if is_pair(step - 1 - 1) else R_PART,
                 )
                 codes = work.tile([P, 2, PAIR * P], U32, tag="codes", bufs=E_LEAD + 1, align_bytes=64)
                 scales = work.tile([P, 2, PAIR * P], U8, tag="scales", bufs=E_LEAD + 1, align_bytes=64)
@@ -325,34 +307,35 @@ def tile_messagepassing_pa_t_kernel(
                     scales[:, parts, :].rearrange("p k c -> p (k c)"),
                 )
                 quantised_in[step - 1] = (codes, scales)
-            if is_pair(step + E_LEAD) or is_pair(step - 2):
+            if is_pair(step + E_LEAD) or is_pair(step - 1):
                 grouped = work.tile([P, 2, PAIR * P, PACK], BF16, tag="grouped", align_bytes=64)
                 grouped_in[step] = grouped
             if is_pair(step + E_LEAD):
                 group_words(e_flipped, grouped[:, E_PART])
-            if 0 < step + 2 < PAIRS:
-                half, j = half_and_j(step + 2)
-                if j == 0:
-                    repeat_h(half)
-                if j % SPREAD_CHUNK == 0:
-                    spread_source_nodes(half, j)
-            if is_pair(step - 4):
-                half, j = half_and_j(step - 4)
+            if is_pair(step - 1):
+                relu(step - 1, grouped[:, R_PART])
+            if is_pair(step - 3):
+                half, j = half_and_j(step - 3)
                 codes, scales = quantised_in[step - 2]
-                messages = second_layer_passes(step - 4, codes[:, R_PART, :], scales[:, R_PART, :])
-                if j + PAIR < NODES:
+                messages = second_layer_passes(step - 3, codes[:, R_PART, :], scales[:, R_PART, :])
+                if step - 3 < PAIRS - 2:
                     mask_on_scalar_add_on_gpsimd(messages[0], half, j)
                     mask_and_add_on_vector(messages[1], half, j + 1)
                 else:
-                    join_sums(half)
+                    if step - 3 == PAIRS - 1:
+                        join_sums(half)
                     mask_and_add_on_vector(messages[0], half, j)
                     mask_and_add_on_vector(messages[1], half, j + 1)
-                    store_half(half)
-            if is_pair(step - 2):
-                relu_and_group(p_flipped, grouped[:, R_PART])
+                    if step - 3 == PAIRS - 1:
+                        store_half(half)
+                if half == 1 and j == 2 * PAIR:
+                    join_sums(0)
+                    store_half(0)
             if is_pair(step):
                 half, j = half_and_j(step)
-                if j == 0:
-                    start_half(half)
                 codes, scales = quantised_in[step - E_LEAD]
                 p_rounded[step] = first_layer(step, codes[:, E_PART, :], scales[:, E_PART, :])
+                if j == 0:
+                    start_sums(half)
+                if half == 0 and j == NODES // 2:
+                    make_source_term(1)

@@ -205,6 +205,7 @@ def tile_messagepassing_pa_t_kernel(
         def first_layer(pair, e_codes, e_scales):
             half, j = half_and_j(pair)
             p_bf = work.tile([P, PAIR, P, PACK], BF16, tag="p_bf")
+            p_rounded[pair] = p_bf
             for s in range(PAIR):
                 cols = slice(s * P, (s + 1) * P)
                 pre = psum.tile([P, PACK, P], F32, tag="bank")
@@ -226,11 +227,12 @@ def tile_messagepassing_pa_t_kernel(
                     .to_broadcast([P, GRAPHS_PER_HALF, NODES, PACK]),
                     op=ADD,
                 )
-            return p_bf
+                if s == 0:
+                    relu(pair, s)
 
-        def relu(pair, grouped):
-            p_bf = p_rounded[pair][:].rearrange("p s c t -> p (s c t)")
-            r = grouped.rearrange("p c t -> p (c t)")
+        def relu(pair, s):
+            r = grouped_in[pair + 1][:, R_PART, s * P : (s + 1) * P, :]
+            p_bf = p_rounded[pair][:, s]
             if pair < PAIRS - 1:
                 nc.scalar.activation(out=r, in_=p_bf, func=RELU)
             else:
@@ -286,6 +288,11 @@ def tile_messagepassing_pa_t_kernel(
         grouped_in = {}
         quantised_in = {}
         p_rounded = {}
+
+        def new_grouped(key):
+            grouped = work.tile([P, 2, PAIR * P, PACK], BF16, tag="grouped", align_bytes=64)
+            grouped_in[key] = grouped
+
         order_columns(W_XJ)
         make_source_term(0)
         order_columns(W_E2)
@@ -307,19 +314,20 @@ def tile_messagepassing_pa_t_kernel(
                     scales[:, parts, :].rearrange("p k c -> p (k c)"),
                 )
                 quantised_in[step - 1] = (codes, scales)
-            if is_pair(step + E_LEAD) or is_pair(step - 1):
-                grouped = work.tile([P, 2, PAIR * P, PACK], BF16, tag="grouped", align_bytes=64)
-                grouped_in[step] = grouped
-            if is_pair(step + E_LEAD):
-                group_words(e_flipped, grouped[:, E_PART])
             if is_pair(step - 1):
-                relu(step - 1, grouped[:, R_PART])
+                relu(step - 1, 1)
+            elif is_pair(step + E_LEAD):
+                new_grouped(step)
+            if is_pair(step + E_LEAD) and not is_pair(step - 3):
+                group_words(e_flipped, grouped_in[step][:, E_PART])
             if is_pair(step - 3):
                 half, j = half_and_j(step - 3)
                 codes, scales = quantised_in[step - 2]
                 messages = second_layer_passes(step - 3, codes[:, R_PART, :], scales[:, R_PART, :])
                 if step - 3 < PAIRS - 2:
                     mask_on_scalar_add_on_gpsimd(messages[0], half, j)
+                    if is_pair(step + E_LEAD):
+                        group_words(e_flipped, grouped_in[step][:, E_PART])
                     mask_and_add_on_vector(messages[1], half, j + 1)
                 else:
                     if step - 3 == PAIRS - 1:
@@ -334,7 +342,8 @@ def tile_messagepassing_pa_t_kernel(
             if is_pair(step):
                 half, j = half_and_j(step)
                 codes, scales = quantised_in[step - E_LEAD]
-                p_rounded[step] = first_layer(step, codes[:, E_PART, :], scales[:, E_PART, :])
+                new_grouped(step + 1)
+                first_layer(step, codes[:, E_PART, :], scales[:, E_PART, :])
                 if j == 0:
                     start_sums(half)
                 if half == 0 and j == NODES // 2:

@@ -314,20 +314,14 @@ def tile_messagepassing_pa_t_kernel(
                     scales[:, parts, :].rearrange("p k c -> p (k c)"),
                 )
                 quantised_in[step - 1] = (codes, scales)
-            if is_pair(step - 1):
-                relu(step - 1, 1)
-            elif is_pair(step + E_LEAD):
+            if not is_pair(step - 1) and is_pair(step + E_LEAD):
                 new_grouped(step)
-            if is_pair(step + E_LEAD) and not is_pair(step - 3):
-                group_words(e_flipped, grouped_in[step][:, E_PART])
             if is_pair(step - 3):
                 half, j = half_and_j(step - 3)
                 codes, scales = quantised_in[step - 2]
                 messages = second_layer_passes(step - 3, codes[:, R_PART, :], scales[:, R_PART, :])
                 if step - 3 < PAIRS - 2:
                     mask_on_scalar_add_on_gpsimd(messages[0], half, j)
-                    if is_pair(step + E_LEAD):
-                        group_words(e_flipped, grouped_in[step][:, E_PART])
                     mask_and_add_on_vector(messages[1], half, j + 1)
                 else:
                     if step - 3 == PAIRS - 1:
@@ -339,6 +333,10 @@ def tile_messagepassing_pa_t_kernel(
                 if half == 1 and j == 2 * PAIR:
                     join_sums(0)
                     store_half(0)
+            if is_pair(step - 1):
+                relu(step - 1, 1)
+            if is_pair(step + E_LEAD):
+                group_words(e_flipped, grouped_in[step][:, E_PART])
             if is_pair(step):
                 half, j = half_and_j(step)
                 codes, scales = quantised_in[step - E_LEAD]

@@ -27,6 +27,7 @@ PAIRS_PER_HALF = NODES // PAIR
 PAIRS = HALVES * PAIRS_PER_HALF
 E_CHUNK = 4
 PSUM_BANKS = 8
+E_RUN = 2
 E_LEAD = 3
 W_XI = 0
 W_XJ = 1
@@ -95,10 +96,10 @@ def tile_messagepassing_pa_t_kernel(
         load_scale_rows(w_planes[:, W_M2, :], w_m2_scales[0])
         while len(e_blocks) < HALVES * NODES:
             load_e(E_CHUNK)
-        b1 = keep.tile([P, PACK], BF16)
-        nc.scalar.dma_start(out=b1[:], in_=b_m1.rearrange("(p t) -> p t", t=PACK))
         mask_bf = keep.tile([P, HALVES, NODES], BF16)
         nc.scalar.dma_start(out=mask_bf[:], in_=mask_rows.rearrange("(s p) j -> p s j", p=P))
+        b1 = keep.tile([P, PACK], BF16)
+        nc.scalar.dma_start(out=b1[:], in_=b_m1.rearrange("(p t) -> p t", t=PACK))
         b2_all = keep.tile([P, H], BF16)
         nc.scalar.dma_start(out=b2_all[:], in_=b_m2.partition_broadcast(P))
 
@@ -149,16 +150,36 @@ def tile_messagepassing_pa_t_kernel(
             cols = slice(t * P, (t + 1) * P)
             return t_words[:, weight, cols], t_planes[:, weight, cols]
 
+        mask_f32 = keep.tile([P, HALVES, NODES], F32)
+        nc.vector.tensor_copy(out=mask_f32[:], in_=mask_bf[:])
+        degree = keep.tile([P, HALVES], F32)
+        nc.vector.tensor_reduce(
+            out=degree[:], in_=mask_f32[:], axis=mybir.AxisListType.X, op=ADD
+        )
+        running = []
+        for half in range(HALVES):
+            by_vector = sums.tile([P, H], F32, tag="by_vector")
+            by_gpsimd = sums.tile([P, H], F32, tag="by_gpsimd")
+            nc.gpsimd.tensor_scalar(
+                out=by_gpsimd[:],
+                in0=b2_all[:],
+                scalar1=degree[:, half : half + 1],
+                scalar2=0.0,
+                op0=MULT,
+                op1=ADD,
+            )
+            nc.gpsimd.tensor_tensor(
+                out=by_gpsimd[:], in0=by_gpsimd[:], in1=h_sb[:, half, :], op=ADD
+            )
+            running.append([by_vector, by_gpsimd])
+
         h_grouped = keep.tile([P, HALVES * P, PACK], BF16, align_bytes=64)
         group_words(flip_input_pair([h_sb[:, 0, :], h_sb[:, 1, :]]), h_grouped[:])
         h_codes = keep.tile([P, HALVES * P], U32, align_bytes=64)
         h_scales = keep.tile([P, HALVES * P], U8, align_bytes=64)
         quantise(h_grouped[:].rearrange("p c t -> p (c t)"), h_codes[:], h_scales[:])
-        mask_f32 = keep.tile([P, HALVES, NODES], F32)
-        degree = keep.tile([P, HALVES], F32)
 
         source_term = {}
-        running = {}
 
         def nodes_of(half):
             cols = slice(half * P, (half + 1) * P)
@@ -177,26 +198,6 @@ def tile_messagepassing_pa_t_kernel(
             )
             source_term[half] = table
 
-        def start_sums(half):
-            nc.vector.tensor_copy(out=mask_f32[:, half, :], in_=mask_bf[:, half, :])
-            nc.vector.tensor_reduce(
-                out=degree[:, half : half + 1],
-                in_=mask_f32[:, half, :],
-                axis=mybir.AxisListType.X,
-                op=ADD,
-            )
-            by_vector = sums.tile([P, H], F32, tag="by_vector")
-            nc.vector.scalar_tensor_tensor(
-                out=by_vector[:],
-                in0=b2_all[:],
-                scalar=degree[:, half : half + 1],
-                in1=h_sb[:, half, :],
-                op0=MULT,
-                op1=ADD,
-            )
-            by_gpsimd = sums.tile([P, H], F32, tag="by_gpsimd")
-            nc.gpsimd.memset(by_gpsimd[:], 0.0)
-            running[half] = [by_vector, by_gpsimd]
 
         def half_and_j(pair):
             half, in_half = divmod(pair, PAIRS_PER_HALF)
@@ -231,7 +232,7 @@ def tile_messagepassing_pa_t_kernel(
                     relu(pair, s)
 
         def relu(pair, s):
-            r = grouped_in[pair + 1][:, R_PART, s * P : (s + 1) * P, :]
+            r = grouped_for(pair + 1)[:, R_PART, s * P : (s + 1) * P, :]
             p_bf = p_rounded[pair][:, s]
             if pair < PAIRS - 1:
                 nc.scalar.activation(out=r, in_=p_bf, func=RELU)
@@ -255,6 +256,15 @@ def tile_messagepassing_pa_t_kernel(
 
         def mask_and_add_on_vector(message, half, j):
             by_vector = running[half][0]
+            if j == 1:
+                nc.vector.tensor_scalar(
+                    out=by_vector[:],
+                    in0=message[:],
+                    scalar1=mask_f32[:, half, j : j + 1],
+                    scalar2=None,
+                    op0=MULT,
+                )
+                return
             nc.vector.scalar_tensor_tensor(
                 out=by_vector[:],
                 in0=message[:],
@@ -272,12 +282,10 @@ def tile_messagepassing_pa_t_kernel(
             )
             nc.gpsimd.tensor_tensor(out=by_gpsimd[:], in0=by_gpsimd[:], in1=masked[:], op=ADD)
 
-        def join_sums(half):
+        def join_and_store(half, engine):
             by_vector, by_gpsimd = running[half]
-            nc.vector.tensor_tensor(out=by_vector[:], in0=by_vector[:], in1=by_gpsimd[:], op=ADD)
-
-        def store_half(half):
-            nc.sync.dma_start(out=out_rows[half * P : (half + 1) * P, :], in_=running[half][0][:])
+            engine.tensor_tensor(out=by_gpsimd[:], in0=by_gpsimd[:], in1=by_vector[:], op=ADD)
+            nc.sync.dma_start(out=out_rows[half * P : (half + 1) * P, :], in_=by_gpsimd[:])
 
         E_PART = 0
         R_PART = 1
@@ -289,18 +297,22 @@ def tile_messagepassing_pa_t_kernel(
         quantised_in = {}
         p_rounded = {}
 
-        def new_grouped(key):
-            grouped = work.tile([P, 2, PAIR * P, PACK], BF16, tag="grouped", align_bytes=64)
-            grouped_in[key] = grouped
+        def grouped_for(step):
+            if step not in grouped_in:
+                grouped = work.tile([P, 2, PAIR * P, PACK], BF16, tag="grouped", align_bytes=64)
+                grouped_in[step] = grouped
+            return grouped_in[step]
 
         order_columns(W_XJ)
         make_source_term(0)
         order_columns(W_E2)
         order_columns(W_XI)
         for step in range(-E_LEAD, PAIRS + 4):
-            if is_pair(step + E_LEAD):
-                first = (step + E_LEAD) * PAIR
-                e_flipped = flip_input_pair(e_blocks[first : first + PAIR])
+            e_flipped = []
+            if is_pair(step + E_LEAD) and (step + E_LEAD) % E_RUN == 0:
+                for k in range(E_RUN):
+                    first = (step + E_LEAD + k) * PAIR
+                    e_flipped.append(flip_input_pair(e_blocks[first : first + PAIR]))
             if step - 1 in grouped_in:
                 parts = slice(
                     E_PART if is_pair(step - 1 + E_LEAD) else R_PART,
@@ -314,35 +326,28 @@ def tile_messagepassing_pa_t_kernel(
                     scales[:, parts, :].rearrange("p k c -> p (k c)"),
                 )
                 quantised_in[step - 1] = (codes, scales)
-            if not is_pair(step - 1) and is_pair(step + E_LEAD):
-                new_grouped(step)
+            if e_flipped:
+                group_words(e_flipped[0], grouped_for(step)[:, E_PART])
             if is_pair(step - 3):
                 half, j = half_and_j(step - 3)
                 codes, scales = quantised_in[step - 2]
                 messages = second_layer_passes(step - 3, codes[:, R_PART, :], scales[:, R_PART, :])
-                if step - 3 < PAIRS - 2:
+                if step - 3 < PAIRS - 1:
                     mask_on_scalar_add_on_gpsimd(messages[0], half, j)
                     mask_and_add_on_vector(messages[1], half, j + 1)
                 else:
-                    if step - 3 == PAIRS - 1:
-                        join_sums(half)
                     mask_and_add_on_vector(messages[0], half, j)
                     mask_and_add_on_vector(messages[1], half, j + 1)
-                    if step - 3 == PAIRS - 1:
-                        store_half(half)
+                    join_and_store(half, nc.vector)
                 if half == 1 and j == 2 * PAIR:
-                    join_sums(0)
-                    store_half(0)
+                    join_and_store(0, nc.gpsimd)
             if is_pair(step - 1):
                 relu(step - 1, 1)
-            if is_pair(step + E_LEAD):
-                group_words(e_flipped, grouped_in[step][:, E_PART])
+            for k in range(1, len(e_flipped)):
+                group_words(e_flipped[k], grouped_for(step + k)[:, E_PART])
             if is_pair(step):
                 half, j = half_and_j(step)
                 codes, scales = quantised_in[step - E_LEAD]
-                new_grouped(step + 1)
                 first_layer(step, codes[:, E_PART, :], scales[:, E_PART, :])
-                if j == 0:
-                    start_sums(half)
                 if half == 0 and j == NODES // 2:
                     make_source_term(1)

@@ -27,7 +27,6 @@ PAIRS_PER_HALF = NODES // PAIR
 PAIRS = HALVES * PAIRS_PER_HALF
 E_CHUNK = 4
 PSUM_BANKS = 8
-E_RUN = 2
 E_LEAD = 3
 W_XI = 0
 W_XJ = 1
@@ -157,27 +156,42 @@ def tile_messagepassing_pa_t_kernel(
             out=degree[:], in_=mask_f32[:], axis=mybir.AxisListType.X, op=ADD
         )
         running = []
-        for half in range(HALVES):
-            by_vector = sums.tile([P, H], F32, tag="by_vector")
-            by_gpsimd = sums.tile([P, H], F32, tag="by_gpsimd")
-            nc.gpsimd.tensor_scalar(
-                out=by_gpsimd[:],
-                in0=b2_all[:],
-                scalar1=degree[:, half : half + 1],
-                scalar2=0.0,
-                op0=MULT,
-                op1=ADD,
-            )
-            nc.gpsimd.tensor_tensor(
-                out=by_gpsimd[:], in0=by_gpsimd[:], in1=h_sb[:, half, :], op=ADD
-            )
-            running.append([by_vector, by_gpsimd])
+
+        def start_sums():
+            for half in range(HALVES):
+                by_vector = sums.tile([P, H], F32, tag="by_vector")
+                by_gpsimd = sums.tile([P, H], F32, tag="by_gpsimd")
+                nc.gpsimd.tensor_scalar(
+                    out=by_gpsimd[:],
+                    in0=b2_all[:],
+                    scalar1=degree[:, half : half + 1],
+                    scalar2=0.0,
+                    op0=MULT,
+                    op1=ADD,
+                )
+                nc.gpsimd.tensor_tensor(
+                    out=by_gpsimd[:], in0=by_gpsimd[:], in1=h_sb[:, half, :], op=ADD
+                )
+                running.append([by_vector, by_gpsimd])
 
         h_grouped = keep.tile([P, HALVES * P, PACK], BF16, align_bytes=64)
         group_words(flip_input_pair([h_sb[:, 0, :], h_sb[:, 1, :]]), h_grouped[:])
         h_codes = keep.tile([P, HALVES * P], U32, align_bytes=64)
         h_scales = keep.tile([P, HALVES * P], U8, align_bytes=64)
+        nc.gpsimd.memset(h_scales[:].bitcast(I32), 0)
         quantise(h_grouped[:].rearrange("p c t -> p (c t)"), h_codes[:], h_scales[:])
+
+        h_codes_twice = keep.tile([P, HALVES, PAIR, P], U32, align_bytes=64)
+        h_scales_twice = keep.tile([P, HALVES, PAIR, P], U8, align_bytes=64)
+        for one, two in ((h_codes, h_codes_twice), (h_scales, h_scales_twice)):
+            words = one[:].bitcast(I32).rearrange("p (s w) -> p s w", s=HALVES)
+            nc.gpsimd.tensor_copy(
+                out=two[:].rearrange("p s r w -> p (s r w)").bitcast(I32).rearrange(
+                    "p (s r w) -> p s r w", s=HALVES, r=PAIR
+                ),
+                in_=words.unsqueeze(2).to_broadcast([P, HALVES, PAIR, words.shape[2]]),
+            )
+        start_sums()
 
         source_term = {}
 
@@ -185,17 +199,29 @@ def tile_messagepassing_pa_t_kernel(
             cols = slice(half * P, (half + 1) * P)
             return h_codes[:, cols], h_scales[:, cols]
 
+        def nodes_twice(half):
+            return (
+                h_codes_twice[:, half].rearrange("p r c -> p (r c)"),
+                h_scales_twice[:, half].rearrange("p r c -> p (r c)"),
+            )
+
         def make_source_term(half):
             a_j = psum.tile([P, PACK, P], F32, tag="bank")
             for t in range(PACK):
                 mx_pass(a_j[:, t, :], channels(W_XJ, t), nodes_of(half), True, True)
-            table = keep.tile([P, P, PACK], F32, name="source_term%d" % half)
-            nc.vector.tensor_tensor(
-                out=table[:],
-                in0=a_j[:].rearrange("p t c -> p c t"),
-                in1=b1[:].unsqueeze(1).to_broadcast([P, P, PACK]),
-                op=ADD,
-            )
+            table = keep.tile([P, 2, P, 2], F32, name="source_term%d" % half)
+            for d in range(2):
+                nc.vector.tensor_tensor(
+                    out=table[:, d].rearrange("p (j b) v -> p j b v", b=GRAPHS_PER_HALF),
+                    in0=a_j[:, 2 * d : 2 * d + 2, :].rearrange(
+                        "p v (b j) -> p j b v", b=GRAPHS_PER_HALF
+                    ),
+                    in1=b1[:, 2 * d : 2 * d + 2]
+                    .unsqueeze(1)
+                    .unsqueeze(1)
+                    .to_broadcast([P, NODES, GRAPHS_PER_HALF, 2]),
+                    op=ADD,
+                )
             source_term[half] = table
 
 
@@ -205,35 +231,27 @@ def tile_messagepassing_pa_t_kernel(
 
         def first_layer(pair, e_codes, e_scales):
             half, j = half_and_j(pair)
-            p_bf = work.tile([P, PAIR, P, PACK], BF16, tag="p_bf")
+            p_bf = work.tile([P, 2, PAIR * P, 2], BF16, tag="p_bf")
             p_rounded[pair] = p_bf
-            for s in range(PAIR):
-                cols = slice(s * P, (s + 1) * P)
-                pre = psum.tile([P, PACK, P], F32, tag="bank")
-                for t in range(PACK):
-                    mx_pass(
-                        pre[:, t, :],
-                        channels(W_E2, t),
-                        (e_codes[:, cols], e_scales[:, cols]),
-                        True,
-                        False,
-                    )
-                    mx_pass(pre[:, t, :], channels(W_XI, t), nodes_of(half), False, True)
+            runs = PAIR * GRAPHS_PER_HALF
+            for d in range(2):
+                pre = psum.tile([P, 2, PAIR * P], F32, tag="bank")
+                for v in range(2):
+                    t = 2 * d + v
+                    mx_pass(pre[:, v, :], channels(W_E2, t), (e_codes, e_scales), True, False)
+                    mx_pass(pre[:, v, :], channels(W_XI, t), nodes_twice(half), False, True)
                 nc.vector.tensor_tensor(
-                    out=p_bf[:, s].rearrange("p (b i) t -> p b i t", b=GRAPHS_PER_HALF),
-                    in0=pre[:].rearrange("p t (b i) -> p b i t", b=GRAPHS_PER_HALF),
-                    in1=source_term[half][:]
-                    .rearrange("p (b j) t -> p b j t", b=GRAPHS_PER_HALF)[:, :, j + s, :]
+                    out=p_bf[:, d].rearrange("p (g i) v -> p g i v", g=runs),
+                    in0=pre[:].rearrange("p v (g i) -> p g i v", g=runs),
+                    in1=source_term[half][:, d, j * GRAPHS_PER_HALF : (j + PAIR) * GRAPHS_PER_HALF, :]
                     .unsqueeze(2)
-                    .to_broadcast([P, GRAPHS_PER_HALF, NODES, PACK]),
+                    .to_broadcast([P, runs, NODES, 2]),
                     op=ADD,
                 )
-                if s == 0:
-                    relu(pair, s)
 
-        def relu(pair, s):
-            r = grouped_for(pair + 1)[:, R_PART, s * P : (s + 1) * P, :]
-            p_bf = p_rounded[pair][:, s]
+        def relu(pair, grouped):
+            p_bf = p_rounded[pair][:].rearrange("p d c v -> p c d v")
+            r = grouped.rearrange("p c (d v) -> p c d v", d=2)
             if pair < PAIRS - 1:
                 nc.scalar.activation(out=r, in_=p_bf, func=RELU)
             else:
@@ -297,22 +315,14 @@ def tile_messagepassing_pa_t_kernel(
         quantised_in = {}
         p_rounded = {}
 
-        def grouped_for(step):
-            if step not in grouped_in:
-                grouped = work.tile([P, 2, PAIR * P, PACK], BF16, tag="grouped", align_bytes=64)
-                grouped_in[step] = grouped
-            return grouped_in[step]
-
         order_columns(W_XJ)
         make_source_term(0)
         order_columns(W_E2)
         order_columns(W_XI)
         for step in range(-E_LEAD, PAIRS + 4):
-            e_flipped = []
-            if is_pair(step + E_LEAD) and (step + E_LEAD) % E_RUN == 0:
-                for k in range(E_RUN):
-                    first = (step + E_LEAD + k) * PAIR
-                    e_flipped.append(flip_input_pair(e_blocks[first : first + PAIR]))
+            if is_pair(step + E_LEAD):
+                first = (step + E_LEAD) * PAIR
+                e_flipped = flip_input_pair(e_blocks[first : first + PAIR])
             if step - 1 in grouped_in:
                 parts = slice(
                     E_PART if is_pair(step - 1 + E_LEAD) else R_PART,
@@ -326,8 +336,11 @@ def tile_messagepassing_pa_t_kernel(
                     scales[:, parts, :].rearrange("p k c -> p (k c)"),
                 )
                 quantised_in[step - 1] = (codes, scales)
-            if e_flipped:
-                group_words(e_flipped[0], grouped_for(step)[:, E_PART])
+            if is_pair(step + E_LEAD) or is_pair(step - 1):
+                grouped = work.tile([P, 2, PAIR * P, PACK], BF16, tag="grouped", align_bytes=64)
+                grouped_in[step] = grouped
+            if is_pair(step + E_LEAD):
+                group_words(e_flipped, grouped[:, E_PART])
             if is_pair(step - 3):
                 half, j = half_and_j(step - 3)
                 codes, scales = quantised_in[step - 2]
@@ -342,9 +355,7 @@ def tile_messagepassing_pa_t_kernel(
                 if half == 1 and j == 2 * PAIR:
                     join_and_store(0, nc.gpsimd)
             if is_pair(step - 1):
-                relu(step - 1, 1)
-            for k in range(1, len(e_flipped)):
-                group_words(e_flipped[k], grouped_for(step + k)[:, E_PART])
+                relu(step - 1, grouped[:, R_PART])
             if is_pair(step):
                 half, j = half_and_j(step)
                 codes, scales = quantised_in[step - E_LEAD]

@@ -11,7 +11,6 @@ U8 = mybir.dt.uint8
 FP8X4 = mybir.dt.float8_e4m3fn_x4
 ADD = mybir.AluOpType.add
 MULT = mybir.AluOpType.mult
-MAX = mybir.AluOpType.max
 RELU = mybir.ActivationFunctionType.Relu
 COPY = mybir.ActivationFunctionType.Copy
 
@@ -25,9 +24,10 @@ GRAPHS_PER_HALF = GRAPHS // HALVES
 PAIR = 2
 PAIRS_PER_HALF = NODES // PAIR
 PAIRS = HALVES * PAIRS_PER_HALF
+LAST_PAIR = PAIRS - 1
 E_CHUNK = 4
 PSUM_BANKS = 8
-E_LEAD = 3
+E_LEAD = 2
 W_XI = 0
 W_XJ = 1
 W_E2 = 2
@@ -47,7 +47,7 @@ def tile_messagepassing_pa_t_kernel(
 
     with ExitStack() as ctx:
         keep = ctx.enter_context(tc.tile_pool(name="keep", bufs=1))
-        e_pool = ctx.enter_context(tc.tile_pool(name="e_pool", bufs=HALVES * NODES // E_CHUNK + 1))
+        e_pool = ctx.enter_context(tc.tile_pool(name="e_pool", bufs=HALVES * NODES // E_CHUNK + 2))
         work = ctx.enter_context(tc.tile_pool(name="work", bufs=3))
         sums = ctx.enter_context(tc.tile_pool(name="sums", bufs=2))
         psum = ctx.enter_context(tc.psum_pool(name="psum", bufs=PSUM_BANKS))
@@ -84,10 +84,11 @@ def tile_messagepassing_pa_t_kernel(
 
         load_w_m1(W_XJ)
         load_scale_rows(w_planes[:, W_XI : W_E2 + 1, :], w_m1_scales.rearrange("g r n -> r g n"))
-        load_e(PAIR)
         load_w_m1(W_E2)
-        load_w_m1(W_XI)
         load_e(PAIR)
+        load_w_m1(W_XI)
+        for pair in range(1, E_CHUNK):
+            load_e(PAIR)
         nc.sync.dma_start(
             out=w_words[:, W_M2, :].bitcast(I32),
             in_=w_m2_words[0].rearrange("p n t -> p (n t)").bitcast(I32),
@@ -99,8 +100,11 @@ def tile_messagepassing_pa_t_kernel(
         nc.scalar.dma_start(out=mask_bf[:], in_=mask_rows.rearrange("(s p) j -> p s j", p=P))
         b1 = keep.tile([P, PACK], BF16)
         nc.scalar.dma_start(out=b1[:], in_=b_m1.rearrange("(p t) -> p t", t=PACK))
-        b2_all = keep.tile([P, H], BF16)
-        nc.scalar.dma_start(out=b2_all[:], in_=b_m2.partition_broadcast(P))
+        b2_row = keep.tile([P, H], BF16)
+        nc.gpsimd.memset(b2_row[:], 0.0)
+        nc.scalar.dma_start(out=b2_row[0:1, :], in_=b_m2.rearrange("(o n) -> o n", o=1))
+        ones = keep.tile([P, P], BF16)
+        nc.gpsimd.memset(ones[:], 1.0)
 
         ident = keep.tile([P, P], F32)
         make_identity(nc, ident[:])
@@ -149,6 +153,20 @@ def tile_messagepassing_pa_t_kernel(
             cols = slice(t * P, (t + 1) * P)
             return t_words[:, weight, cols], t_planes[:, weight, cols]
 
+        h_grouped = keep.tile([P, HALVES * P, PACK], BF16, align_bytes=64)
+        group_words(flip_input_pair([h_sb[:, 0, :], h_sb[:, 1, :]]), h_grouped[:])
+        h_codes = keep.tile([P, HALVES, PAIR, P], U32, align_bytes=64)
+        h_scales = keep.tile([P, HALVES, PAIR, P], U8, align_bytes=64)
+        nc.gpsimd.memset(h_scales[:].bitcast(I32), 0)
+        for half in range(HALVES):
+            quantise(
+                h_grouped[:, half * P : (half + 1) * P, :].rearrange("p c t -> p (c t)"),
+                h_codes[:, half, 0, :],
+                h_scales[:, half, 0, :],
+            )
+
+        order_columns(W_XJ)
+
         mask_f32 = keep.tile([P, HALVES, NODES], F32)
         nc.vector.tensor_copy(out=mask_f32[:], in_=mask_bf[:])
         degree = keep.tile([P, HALVES], F32)
@@ -156,53 +174,37 @@ def tile_messagepassing_pa_t_kernel(
             out=degree[:], in_=mask_f32[:], axis=mybir.AxisListType.X, op=ADD
         )
         running = []
-
-        def start_sums():
-            for half in range(HALVES):
-                by_vector = sums.tile([P, H], F32, tag="by_vector")
-                by_gpsimd = sums.tile([P, H], F32, tag="by_gpsimd")
-                nc.gpsimd.tensor_scalar(
-                    out=by_gpsimd[:],
-                    in0=b2_all[:],
-                    scalar1=degree[:, half : half + 1],
-                    scalar2=0.0,
-                    op0=MULT,
-                    op1=ADD,
-                )
-                nc.gpsimd.tensor_tensor(
-                    out=by_gpsimd[:], in0=by_gpsimd[:], in1=h_sb[:, half, :], op=ADD
-                )
-                running.append([by_vector, by_gpsimd])
-
-        h_grouped = keep.tile([P, HALVES * P, PACK], BF16, align_bytes=64)
-        group_words(flip_input_pair([h_sb[:, 0, :], h_sb[:, 1, :]]), h_grouped[:])
-        h_codes = keep.tile([P, HALVES * P], U32, align_bytes=64)
-        h_scales = keep.tile([P, HALVES * P], U8, align_bytes=64)
-        nc.gpsimd.memset(h_scales[:].bitcast(I32), 0)
-        quantise(h_grouped[:].rearrange("p c t -> p (c t)"), h_codes[:], h_scales[:])
-
-        h_codes_twice = keep.tile([P, HALVES, PAIR, P], U32, align_bytes=64)
-        h_scales_twice = keep.tile([P, HALVES, PAIR, P], U8, align_bytes=64)
-        for one, two in ((h_codes, h_codes_twice), (h_scales, h_scales_twice)):
-            words = one[:].bitcast(I32).rearrange("p (s w) -> p s w", s=HALVES)
-            nc.gpsimd.tensor_copy(
-                out=two[:].rearrange("p s r w -> p (s r w)").bitcast(I32).rearrange(
-                    "p (s r w) -> p s r w", s=HALVES, r=PAIR
-                ),
-                in_=words.unsqueeze(2).to_broadcast([P, HALVES, PAIR, words.shape[2]]),
+        b2_all = psum.tile([P, H], F32, tag="bank")
+        nc.tensor.matmul(out=b2_all[:], lhsT=ones[:], rhs=b2_row[:], start=True, stop=True)
+        for half in range(HALVES):
+            by_vector = sums.tile([P, H], F32, tag="by_vector")
+            by_gpsimd = sums.tile([P, H], F32, tag="by_gpsimd")
+            nc.scalar.activation(
+                out=by_gpsimd[:], in_=b2_all[:], func=COPY, scale=degree[:, half : half + 1]
             )
-        start_sums()
+            running.append([by_vector, by_gpsimd])
+
+        def add_h(half):
+            by_gpsimd = running[half][1]
+            nc.gpsimd.tensor_tensor(
+                out=by_gpsimd[:], in0=by_gpsimd[:], in1=h_sb[:, half, :], op=ADD
+            )
+
+        def repeat_h():
+            for plane in (h_codes, h_scales):
+                nc.vector.tensor_copy(
+                    out=plane[:, :, 1, :].bitcast(I32), in_=plane[:, :, 0, :].bitcast(I32)
+                )
 
         source_term = {}
 
         def nodes_of(half):
-            cols = slice(half * P, (half + 1) * P)
-            return h_codes[:, cols], h_scales[:, cols]
+            return h_codes[:, half, 0, :], h_scales[:, half, 0, :]
 
         def nodes_twice(half):
             return (
-                h_codes_twice[:, half].rearrange("p r c -> p (r c)"),
-                h_scales_twice[:, half].rearrange("p r c -> p (r c)"),
+                h_codes[:, half].rearrange("p r c -> p (r c)"),
+                h_scales[:, half].rearrange("p r c -> p (r c)"),
             )
 
         def make_source_term(half):
@@ -252,25 +254,45 @@ def tile_messagepassing_pa_t_kernel(
         def relu(pair, grouped):
             p_bf = p_rounded[pair][:].rearrange("p d c v -> p c d v")
             r = grouped.rearrange("p c (d v) -> p c d v", d=2)
-            if pair < PAIRS - 1:
-                nc.scalar.activation(out=r, in_=p_bf, func=RELU)
-            else:
-                nc.vector.tensor_scalar(out=r, in0=p_bf, scalar1=0.0, scalar2=None, op0=MAX)
+            nc.scalar.activation(out=r, in_=p_bf, func=RELU)
 
-        def second_layer_passes(pair, r_codes, r_scales):
-            messages = []
-            for s in range(PAIR):
-                cols = slice(s * P, (s + 1) * P)
-                message = psum.tile([P, H], F32, tag="bank")
-                mx_pass(
-                    message[:],
-                    (r_codes[:, cols], r_scales[:, cols]),
-                    (w_words[:, W_M2, :], w_planes[:, W_M2, :]),
-                    True,
-                    True,
+        def first_layer_of_last_pair(s, e_codes, e_scales):
+            half, j = half_and_j(LAST_PAIR)
+            p_bf = keep.tile([P, 2, P, 2], BF16, name="last_p%d" % s)
+            r = keep.tile([P, P, PACK], BF16, name="last_r%d" % s, align_bytes=64)
+            sources = slice((j + s) * GRAPHS_PER_HALF, (j + s + 1) * GRAPHS_PER_HALF)
+            pre = psum.tile([P, PACK, P], F32, tag="bank")
+            for t in range(PACK):
+                mx_pass(pre[:, t, :], channels(W_E2, t), (e_codes, e_scales), True, False)
+                mx_pass(pre[:, t, :], channels(W_XI, t), nodes_of(half), False, True)
+            for d in range(2):
+                nc.vector.tensor_tensor(
+                    out=p_bf[:, d].rearrange("p (b i) v -> p b i v", b=GRAPHS_PER_HALF),
+                    in0=pre[:, 2 * d : 2 * d + 2, :].rearrange(
+                        "p v (b i) -> p b i v", b=GRAPHS_PER_HALF
+                    ),
+                    in1=source_term[half][:, d, sources, :]
+                    .unsqueeze(2)
+                    .to_broadcast([P, GRAPHS_PER_HALF, NODES, 2]),
+                    op=ADD,
                 )
-                messages.append(message)
-            return messages
+            nc.scalar.activation(
+                out=r[:].rearrange("p c (d v) -> p c d v", d=2),
+                in_=p_bf[:].rearrange("p d c v -> p c d v"),
+                func=RELU,
+            )
+            return r
+
+        def quantise_last(s, r):
+            codes = keep.tile([P, P], U32, name="last_codes%d" % s, align_bytes=64)
+            scales = keep.tile([P, P], U8, name="last_scales%d" % s, align_bytes=64)
+            quantise(r[:].rearrange("p c t -> p (c t)"), codes[:], scales[:])
+            return codes[:], scales[:]
+
+        def second_layer_pass(r):
+            message = psum.tile([P, H], F32, tag="bank")
+            mx_pass(message[:], r, (w_words[:, W_M2, :], w_planes[:, W_M2, :]), True, True)
+            return message
 
         def mask_and_add_on_vector(message, half, j):
             by_vector = running[half][0]
@@ -300,10 +322,14 @@ def tile_messagepassing_pa_t_kernel(
             )
             nc.gpsimd.tensor_tensor(out=by_gpsimd[:], in0=by_gpsimd[:], in1=masked[:], op=ADD)
 
-        def join_and_store(half, engine):
+        def join_and_store(half, engine, cols):
             by_vector, by_gpsimd = running[half]
-            engine.tensor_tensor(out=by_gpsimd[:], in0=by_gpsimd[:], in1=by_vector[:], op=ADD)
-            nc.sync.dma_start(out=out_rows[half * P : (half + 1) * P, :], in_=by_gpsimd[:])
+            engine.tensor_tensor(
+                out=by_gpsimd[:, cols], in0=by_gpsimd[:, cols], in1=by_vector[:, cols], op=ADD
+            )
+            nc.sync.dma_start(
+                out=out_rows[half * P : (half + 1) * P, cols], in_=by_gpsimd[:, cols]
+            )
 
         E_PART = 0
         R_PART = 1
@@ -315,50 +341,77 @@ def tile_messagepassing_pa_t_kernel(
         quantised_in = {}
         p_rounded = {}
 
-        order_columns(W_XJ)
-        make_source_term(0)
+        def new_grouped(step):
+            grouped = work.tile([P, 2, PAIR * P, PACK], BF16, tag="grouped", align_bytes=64)
+            grouped_in[step] = grouped
+
+        def quantise_grouped(step):
+            parts = slice(
+                E_PART if is_pair(step + E_LEAD) else R_PART,
+                R_PART + 1 if is_pair(step - 1) else R_PART,
+            )
+            codes = work.tile([P, 2, PAIR * P], U32, tag="codes", bufs=E_LEAD + 1, align_bytes=64)
+            scales = work.tile([P, 2, PAIR * P], U8, tag="scales", bufs=E_LEAD + 1, align_bytes=64)
+            quantise(
+                grouped_in[step][:, parts].rearrange("p k c t -> p (k c t)"),
+                codes[:, parts, :].rearrange("p k c -> p (k c)"),
+                scales[:, parts, :].rearrange("p k c -> p (k c)"),
+            )
+            quantised_in[step] = (codes, scales)
+
+        def second_layer(pair):
+            half, j = half_and_j(pair)
+            codes, scales = quantised_in[pair + 1]
+            messages = []
+            for s in range(PAIR):
+                cols = slice(s * P, (s + 1) * P)
+                messages.append(second_layer_pass((codes[:, R_PART, cols], scales[:, R_PART, cols])))
+            mask_on_scalar_add_on_gpsimd(messages[0], half, j)
+            mask_and_add_on_vector(messages[1], half, j + 1)
+
         order_columns(W_E2)
+        repeat_h()
+        make_source_term(0)
         order_columns(W_XI)
-        for step in range(-E_LEAD, PAIRS + 4):
+        for step in range(-E_LEAD, LAST_PAIR):
             if is_pair(step + E_LEAD):
                 first = (step + E_LEAD) * PAIR
                 e_flipped = flip_input_pair(e_blocks[first : first + PAIR])
             if step - 1 in grouped_in:
-                parts = slice(
-                    E_PART if is_pair(step - 1 + E_LEAD) else R_PART,
-                    R_PART + 1 if is_pair(step - 1 - 1) else R_PART,
-                )
-                codes = work.tile([P, 2, PAIR * P], U32, tag="codes", bufs=E_LEAD + 1, align_bytes=64)
-                scales = work.tile([P, 2, PAIR * P], U8, tag="scales", bufs=E_LEAD + 1, align_bytes=64)
-                quantise(
-                    grouped_in[step - 1][:, parts].rearrange("p k c t -> p (k c t)"),
-                    codes[:, parts, :].rearrange("p k c -> p (k c)"),
-                    scales[:, parts, :].rearrange("p k c -> p (k c)"),
-                )
-                quantised_in[step - 1] = (codes, scales)
-            if is_pair(step + E_LEAD) or is_pair(step - 1):
-                grouped = work.tile([P, 2, PAIR * P, PACK], BF16, tag="grouped", align_bytes=64)
-                grouped_in[step] = grouped
+                quantise_grouped(step - 1)
+            new_grouped(step)
             if is_pair(step + E_LEAD):
-                group_words(e_flipped, grouped[:, E_PART])
+                group_words(e_flipped, grouped_in[step][:, E_PART])
             if is_pair(step - 3):
-                half, j = half_and_j(step - 3)
-                codes, scales = quantised_in[step - 2]
-                messages = second_layer_passes(step - 3, codes[:, R_PART, :], scales[:, R_PART, :])
-                if step - 3 < PAIRS - 1:
-                    mask_on_scalar_add_on_gpsimd(messages[0], half, j)
-                    mask_and_add_on_vector(messages[1], half, j + 1)
-                else:
-                    mask_and_add_on_vector(messages[0], half, j)
-                    mask_and_add_on_vector(messages[1], half, j + 1)
-                    join_and_store(half, nc.vector)
-                if half == 1 and j == 2 * PAIR:
-                    join_and_store(0, nc.gpsimd)
+                second_layer(step - 3)
+                if step - 3 in (0, 2):
+                    add_h((step - 3) // 2)
+                if step - 3 == PAIRS_PER_HALF + 2:
+                    join_and_store(0, nc.gpsimd, slice(0, H))
             if is_pair(step - 1):
-                relu(step - 1, grouped[:, R_PART])
+                relu(step - 1, grouped_in[step][:, R_PART])
             if is_pair(step):
-                half, j = half_and_j(step)
                 codes, scales = quantised_in[step - E_LEAD]
                 first_layer(step, codes[:, E_PART, :], scales[:, E_PART, :])
-                if half == 0 and j == NODES // 2:
+                if step == PAIRS_PER_HALF // 2:
                     make_source_term(1)
+
+        codes, scales = quantised_in[LAST_PAIR - E_LEAD]
+        quantise_grouped(LAST_PAIR - 1)
+        second_layer(LAST_PAIR - 3)
+        new_grouped(LAST_PAIR)
+        relu(LAST_PAIR - 1, grouped_in[LAST_PAIR][:, R_PART])
+        first, second = (slice(s * P, (s + 1) * P) for s in range(PAIR))
+        second_layer(LAST_PAIR - 2)
+        r_first = first_layer_of_last_pair(0, codes[:, E_PART, first], scales[:, E_PART, first])
+        quantise_grouped(LAST_PAIR)
+        r_second = first_layer_of_last_pair(1, codes[:, E_PART, second], scales[:, E_PART, second])
+        first_quantised = quantise_last(0, r_first)
+        second_layer(LAST_PAIR - 1)
+        half, j = half_and_j(LAST_PAIR)
+        message = second_layer_pass(first_quantised)
+        second_quantised = quantise_last(1, r_second)
+        mask_and_add_on_vector(message, half, j)
+        mask_and_add_on_vector(second_layer_pass(second_quantised), half, j + 1)
+        for piece in range(2):
+            join_and_store(half, nc.vector, slice(piece * H // 2, (piece + 1) * H // 2))

@@ -27,6 +27,7 @@ PAIRS = HALVES * PAIRS_PER_HALF
 LAST_PAIR = PAIRS - 1
 E_CHUNK = 4
 PSUM_BANKS = 8
+FLIP_BANKS = 2
 E_LEAD = 2
 W_XI = 0
 W_XJ = 1
@@ -50,7 +51,8 @@ def tile_messagepassing_pa_t_kernel(
         e_pool = ctx.enter_context(tc.tile_pool(name="e_pool", bufs=HALVES * NODES // E_CHUNK + 2))
         work = ctx.enter_context(tc.tile_pool(name="work", bufs=3))
         sums = ctx.enter_context(tc.tile_pool(name="sums", bufs=2))
-        psum = ctx.enter_context(tc.psum_pool(name="psum", bufs=PSUM_BANKS))
+        flips = ctx.enter_context(tc.psum_pool(name="flips", bufs=FLIP_BANKS))
+        psum = ctx.enter_context(tc.psum_pool(name="psum", bufs=PSUM_BANKS - FLIP_BANKS))
         ctx.enter_context(tc.manual_schedule())
 
         w_planes = keep.tile([P, 4, H], U8, align_bytes=64)
@@ -110,7 +112,7 @@ def tile_messagepassing_pa_t_kernel(
         make_identity(nc, ident[:])
 
         def flip_input_pair(sources):
-            flipped = psum.tile([P, 2, PAIR * P], F32, tag="bank")
+            flipped = flips.tile([P, 2, PAIR * P], F32)
             for s in range(PAIR):
                 words = sources[s].bitcast(F32)
                 for u in range(2):
@@ -337,6 +339,12 @@ def tile_messagepassing_pa_t_kernel(
         def is_pair(pair):
             return 0 <= pair < PAIRS
 
+        def e_run(pair):
+            if pair == 0:
+                return [0]
+            return [q for q in (pair, pair + 1) if pair % 2 == 1 and is_pair(q)]
+
+        e_flipped = {}
         grouped_in = {}
         quantised_in = {}
         p_rounded = {}
@@ -374,14 +382,13 @@ def tile_messagepassing_pa_t_kernel(
         make_source_term(0)
         order_columns(W_XI)
         for step in range(-E_LEAD, LAST_PAIR):
-            if is_pair(step + E_LEAD):
-                first = (step + E_LEAD) * PAIR
-                e_flipped = flip_input_pair(e_blocks[first : first + PAIR])
+            for pair in e_run(step + E_LEAD):
+                e_flipped[pair] = flip_input_pair(e_blocks[pair * PAIR : (pair + 1) * PAIR])
             if step - 1 in grouped_in:
                 quantise_grouped(step - 1)
             new_grouped(step)
             if is_pair(step + E_LEAD):
-                group_words(e_flipped, grouped_in[step][:, E_PART])
+                group_words(e_flipped[step + E_LEAD], grouped_in[step][:, E_PART])
             if is_pair(step - 3):
                 second_layer(step - 3)
                 if step - 3 in (0, 2):

@@ -84,9 +84,9 @@ def tile_messagepassing_pa_t_kernel(
             )
             e_blocks.extend([e_sb[:, s, :] for s in range(blocks)])
 
-        load_w_m1(W_XJ)
-        load_scale_rows(w_planes[:, W_XI : W_E2 + 1, :], w_m1_scales.rearrange("g r n -> r g n"))
         load_w_m1(W_E2)
+        load_scale_rows(w_planes[:, W_XI : W_E2 + 1, :], w_m1_scales.rearrange("g r n -> r g n"))
+        load_w_m1(W_XJ)
         load_e(PAIR)
         load_w_m1(W_XI)
         for pair in range(1, E_CHUNK):
@@ -138,22 +138,24 @@ def tile_messagepassing_pa_t_kernel(
                 stop=stop,
             )
 
-        t_words = keep.tile([P, 3, H], U32, align_bytes=64)
-        t_planes = keep.tile([P, 3, H], U8, align_bytes=64)
+        t_words = keep.tile([P, 2, H], U32, align_bytes=64)
+        t_planes = keep.tile([P, 2, H], U8, align_bytes=64)
+        t_place = {W_XI: 0, W_E2: 1}
 
         def order_columns(weight):
+            place = t_place[weight]
             nc.vector.tensor_copy(
-                out=t_words[:, weight, :].bitcast(I32).rearrange("p (t m) -> p m t", t=PACK),
+                out=t_words[:, place, :].bitcast(I32).rearrange("p (t m) -> p m t", t=PACK),
                 in_=w_words[:, weight, :].bitcast(I32).rearrange("p (m t) -> p m t", t=PACK),
             )
             nc.vector.tensor_copy(
-                out=t_planes[:, weight, :].rearrange("p (t m) -> p m t", t=PACK),
+                out=t_planes[:, place, :].rearrange("p (t m) -> p m t", t=PACK),
                 in_=w_planes[:, weight, :].rearrange("p (m t) -> p m t", t=PACK),
             )
 
         def channels(weight, t):
             cols = slice(t * P, (t + 1) * P)
-            return t_words[:, weight, cols], t_planes[:, weight, cols]
+            return t_words[:, t_place[weight], cols], t_planes[:, t_place[weight], cols]
 
         h_grouped = keep.tile([P, HALVES * P, PACK], BF16, align_bytes=64)
         group_words(flip_input_pair([h_sb[:, 0, :], h_sb[:, 1, :]]), h_grouped[:])
@@ -167,7 +169,7 @@ def tile_messagepassing_pa_t_kernel(
                 h_scales[:, half, 0, :],
             )
 
-        order_columns(W_XJ)
+        order_columns(W_E2)
 
         mask_f32 = keep.tile([P, HALVES, NODES], F32)
         nc.vector.tensor_copy(out=mask_f32[:], in_=mask_bf[:])
@@ -178,13 +180,19 @@ def tile_messagepassing_pa_t_kernel(
         running = []
         b2_all = psum.tile([P, H], F32, tag="bank")
         nc.tensor.matmul(out=b2_all[:], lhsT=ones[:], rhs=b2_row[:], start=True, stop=True)
-        for half in range(HALVES):
-            by_vector = sums.tile([P, H], F32, tag="by_vector")
-            by_gpsimd = sums.tile([P, H], F32, tag="by_gpsimd")
-            nc.scalar.activation(
-                out=by_gpsimd[:], in_=b2_all[:], func=COPY, scale=degree[:, half : half + 1]
-            )
-            running.append([by_vector, by_gpsimd])
+
+        def start_sums():
+            for half in range(HALVES):
+                by_vector = sums.tile([P, H], F32, tag="by_vector")
+                by_gpsimd = sums.tile([P, H], F32, tag="by_gpsimd")
+                nc.vector.tensor_scalar(
+                    out=by_gpsimd[:],
+                    in0=b2_all[:],
+                    scalar1=degree[:, half : half + 1],
+                    scalar2=None,
+                    op0=MULT,
+                )
+                running.append([by_vector, by_gpsimd])
 
         def add_h(half):
             by_gpsimd = running[half][1]
@@ -209,10 +217,22 @@ def tile_messagepassing_pa_t_kernel(
                 h_scales[:, half].rearrange("p r c -> p (r c)"),
             )
 
-        def make_source_term(half):
+        source_rows = {}
+
+        def make_source_rows(half):
+            product = psum.tile([P, H], F32, tag="bank")
+            mx_pass(product[:], nodes_of(half), (w_words[:, W_XJ, :], w_planes[:, W_XJ, :]), True, True)
+            rows = keep.tile([P, H], F32, name="source_rows%d" % half)
+            nc.scalar.copy(out=rows[:], in_=product[:])
+            source_rows[half] = rows
+
+        def flip_source_rows(half):
             a_j = psum.tile([P, PACK, P], F32, tag="bank")
             for t in range(PACK):
-                mx_pass(a_j[:, t, :], channels(W_XJ, t), nodes_of(half), True, True)
+                nc.tensor.transpose(a_j[:, t, :], source_rows[half][:, t:H:PACK], ident[:])
+            return a_j
+
+        def make_source_term(half, a_j):
             table = keep.tile([P, 2, P, 2], F32, name="source_term%d" % half)
             for d in range(2):
                 nc.vector.tensor_tensor(
@@ -340,11 +360,18 @@ def tile_messagepassing_pa_t_kernel(
             return 0 <= pair < PAIRS
 
         def e_run(pair):
-            if pair == 0:
-                return [0]
-            return [q for q in (pair, pair + 1) if pair % 2 == 1 and is_pair(q)]
+            if pair < E_LEAD:
+                return [pair]
+            return [q for q in (pair, pair + 1) if pair % 2 == 0 and pair > E_LEAD and is_pair(q)]
 
         e_flipped = {}
+
+        def flip_e(pair):
+            e_flipped[pair] = flip_input_pair(e_blocks[pair * PAIR : (pair + 1) * PAIR])
+
+        def group_e(step):
+            group_words(e_flipped[step + E_LEAD], grouped_in[step][:, E_PART])
+
         grouped_in = {}
         quantised_in = {}
         p_rounded = {}
@@ -377,18 +404,22 @@ def tile_messagepassing_pa_t_kernel(
             mask_on_scalar_add_on_gpsimd(messages[0], half, j)
             mask_and_add_on_vector(messages[1], half, j + 1)
 
-        order_columns(W_E2)
+        make_source_rows(0)
         repeat_h()
-        make_source_term(0)
         order_columns(W_XI)
+        start_sums()
         for step in range(-E_LEAD, LAST_PAIR):
             for pair in e_run(step + E_LEAD):
-                e_flipped[pair] = flip_input_pair(e_blocks[pair * PAIR : (pair + 1) * PAIR])
+                flip_e(pair)
             if step - 1 in grouped_in:
                 quantise_grouped(step - 1)
             new_grouped(step)
-            if is_pair(step + E_LEAD):
-                group_words(e_flipped[step + E_LEAD], grouped_in[step][:, E_PART])
+            if is_pair(step + E_LEAD) and step != 0:
+                group_e(step)
+            if step == -E_LEAD:
+                source_columns = flip_source_rows(0)
+            if step == 1 - E_LEAD:
+                make_source_term(0, source_columns)
             if is_pair(step - 3):
                 second_layer(step - 3)
                 if step - 3 in (0, 2):
@@ -400,8 +431,14 @@ def tile_messagepassing_pa_t_kernel(
             if is_pair(step):
                 codes, scales = quantised_in[step - E_LEAD]
                 first_layer(step, codes[:, E_PART, :], scales[:, E_PART, :])
+                if step == 0:
+                    flip_e(E_LEAD)
+                    flip_e(E_LEAD + 1)
+                    group_e(0)
                 if step == PAIRS_PER_HALF // 2:
-                    make_source_term(1)
+                    make_source_rows(1)
+                if step == PAIRS_PER_HALF // 2 + 1:
+                    make_source_term(1, flip_source_rows(1))
 
         codes, scales = quantised_in[LAST_PAIR - E_LEAD]
         quantise_grouped(LAST_PAIR - 1)
@@ -409,9 +446,9 @@ def tile_messagepassing_pa_t_kernel(
         new_grouped(LAST_PAIR)
         relu(LAST_PAIR - 1, grouped_in[LAST_PAIR][:, R_PART])
         first, second = (slice(s * P, (s + 1) * P) for s in range(PAIR))
-        second_layer(LAST_PAIR - 2)
         r_first = first_layer_of_last_pair(0, codes[:, E_PART, first], scales[:, E_PART, first])
         quantise_grouped(LAST_PAIR)
+        second_layer(LAST_PAIR - 2)
         r_second = first_layer_of_last_pair(1, codes[:, E_PART, second], scales[:, E_PART, second])
         first_quantised = quantise_last(0, r_first)
         second_layer(LAST_PAIR - 1)

from contextlib import ExitStack

import concourse.mybir as mybir
from concourse.masks import make_identity

F32 = mybir.dt.float32
BF16 = mybir.dt.bfloat16
I32 = mybir.dt.int32
U32 = mybir.dt.uint32
U8 = mybir.dt.uint8
FP8X4 = mybir.dt.float8_e4m3fn_x4
ADD = mybir.AluOpType.add
MULT = mybir.AluOpType.mult
RELU = mybir.ActivationFunctionType.Relu
COPY = mybir.ActivationFunctionType.Copy

GRAPHS = 8
NODES = 32
H = 512
P = 128
PACK = 4
HALVES = GRAPHS * NODES // P
GRAPHS_PER_HALF = GRAPHS // HALVES
PAIR = 2
PAIRS_PER_HALF = NODES // PAIR
PAIRS = HALVES * PAIRS_PER_HALF
LAST_PAIR = PAIRS - 1
E_CHUNK = 4
PSUM_BANKS = 8
FLIP_BANKS = 2
E_LEAD = 2
W_XI = 0
W_XJ = 1
W_E2 = 2
W_M2 = 3

FLOPS = 2 * H * H * (2 * GRAPHS * NODES * NODES + 2 * GRAPHS * NODES)


def tile_messagepassing_pa_t_kernel(
    tc, h, e, adj_mask, w_m1_words, w_m1_scales, b_m1, w_m2_words, w_m2_scales, b_m2, out
):
    nc = tc.nc
    h_rows = h.rearrange("b i k -> (b i) k")
    e_rows = e.rearrange("b i j k -> (b i) j k")
    mask_rows = adj_mask.rearrange("b i j o -> (b i) (j o)")
    out_rows = out.rearrange("b i n -> (b i) n")

    with ExitStack() as ctx:
        keep = ctx.enter_context(tc.tile_pool(name="keep", bufs=1))
        e_pool = ctx.enter_context(tc.tile_pool(name="e_pool", bufs=HALVES * NODES // E_CHUNK + 2))
        work = ctx.enter_context(tc.tile_pool(name="work", bufs=3))
        sums = ctx.enter_context(tc.tile_pool(name="sums", bufs=2))
        flips = ctx.enter_context(tc.psum_pool(name="flips", bufs=FLIP_BANKS))
        psum = ctx.enter_context(tc.psum_pool(name="psum", bufs=PSUM_BANKS - FLIP_BANKS))
        ctx.enter_context(tc.manual_schedule())

        w_planes = keep.tile([P, 4, H], U8, align_bytes=64)
        nc.vector.memset(w_planes[:].bitcast(I32), 0)
        w_words = keep.tile([P, 4, H], U32, align_bytes=64)
        h_sb = keep.tile([P, HALVES, H], BF16)
        nc.sync.dma_start(out=h_sb[:], in_=h_rows.rearrange("(s p) k -> p s k", p=P))

        def load_scale_rows(planes, scale_rows):
            for quad in range(4):
                nc.sync.dma_start(
                    out=planes[32 * quad : 32 * quad + 4].bitcast(I32),
                    in_=scale_rows[4 * quad : 4 * quad + 4].bitcast(I32),
                )

        def load_w_m1(weight):
            nc.sync.dma_start(
                out=w_words[:, weight, :].bitcast(I32),
                in_=w_m1_words[weight].rearrange("p n t -> p (n t)").bitcast(I32),
            )

        e_blocks = []

        def load_e(blocks):
            half, j = divmod(len(e_blocks), NODES)
            e_sb = e_pool.tile([P, blocks, H], BF16)
            nc.sync.dma_start(
                out=e_sb[:], in_=e_rows[half * P : (half + 1) * P, j : j + blocks, :]
            )
            e_blocks.extend([e_sb[:, s, :] for s in range(blocks)])

        load_w_m1(W_E2)
        load_scale_rows(w_planes[:, W_XI : W_E2 + 1, :], w_m1_scales.rearrange("g r n -> r g n"))
        load_w_m1(W_XJ)
        load_e(PAIR)
        load_w_m1(W_XI)
        for pair in range(1, E_CHUNK):
            load_e(PAIR)
        nc.sync.dma_start(
            out=w_words[:, W_M2, :].bitcast(I32),
            in_=w_m2_words[0].rearrange("p n t -> p (n t)").bitcast(I32),
        )
        load_scale_rows(w_planes[:, W_M2, :], w_m2_scales[0])
        while len(e_blocks) < HALVES * NODES:
            load_e(E_CHUNK)
        mask_bf = keep.tile([P, HALVES, NODES], BF16)
        nc.scalar.dma_start(out=mask_bf[:], in_=mask_rows.rearrange("(s p) j -> p s j", p=P))
        b1 = keep.tile([P, PACK], BF16)
        nc.scalar.dma_start(out=b1[:], in_=b_m1.rearrange("(p t) -> p t", t=PACK))
        b2_row = keep.tile([P, H], BF16)
        nc.gpsimd.memset(b2_row[:], 0.0)
        nc.scalar.dma_start(out=b2_row[0:1, :], in_=b_m2.rearrange("(o n) -> o n", o=1))
        ones = keep.tile([P, P], BF16)
        nc.gpsimd.memset(ones[:], 1.0)

        ident = keep.tile([P, P], F32)
        make_identity(nc, ident[:])

        def flip_input_pair(sources):
            flipped = flips.tile([P, 2, PAIR * P], F32)
            for s in range(PAIR):
                words = sources[s].bitcast(F32)
                for u in range(2):
                    nc.tensor.transpose(
                        flipped[:, u, s * P : (s + 1) * P], words[:, u : H // 2 : 2], ident[:]
                    )
            return flipped

        def group_words(flipped, grouped):
            nc.scalar.copy(out=grouped.bitcast(F32), in_=flipped[:].rearrange("p u c -> p c u"))

        def quantise(grouped, codes, scales):
            nc.vector.quantize_mx(out=codes.bitcast(FP8X4), scales=scales, in_=grouped)

        def mx_pass(acc, left, right, start, stop):
            nc.tensor.matmul_mx(
                out=acc,
                lhsT=left[0].bitcast(FP8X4),
                lhsT_scale=left[1],
                rhs=right[0].bitcast(FP8X4),
                rhs_scale=right[1],
                start=start,
                stop=stop,
            )

        t_words = keep.tile([P, 2, H], U32, align_bytes=64)
        t_planes = keep.tile([P, 2, H], U8, align_bytes=64)
        t_place = {W_XI: 0, W_E2: 1}

        def order_columns(weight):
            place = t_place[weight]
            nc.vector.tensor_copy(
                out=t_words[:, place, :].bitcast(I32).rearrange("p (t m) -> p m t", t=PACK),
                in_=w_words[:, weight, :].bitcast(I32).rearrange("p (m t) -> p m t", t=PACK),
            )
            nc.vector.tensor_copy(
                out=t_planes[:, place, :].rearrange("p (t m) -> p m t", t=PACK),
                in_=w_planes[:, weight, :].rearrange("p (m t) -> p m t", t=PACK),
            )

        def channels(weight, t):
            cols = slice(t * P, (t + 1) * P)
            return t_words[:, t_place[weight], cols], t_planes[:, t_place[weight], cols]

        h_grouped = keep.tile([P, HALVES * P, PACK], BF16, align_bytes=64)
        group_words(flip_input_pair([h_sb[:, 0, :], h_sb[:, 1, :]]), h_grouped[:])
        h_codes = keep.tile([P, HALVES, PAIR, P], U32, align_bytes=64)
        h_scales = keep.tile([P, HALVES, PAIR, P], U8, align_bytes=64)
        nc.gpsimd.memset(h_scales[:].bitcast(I32), 0)
        for half in range(HALVES):
            quantise(
                h_grouped[:, half * P : (half + 1) * P, :].rearrange("p c t -> p (c t)"),
                h_codes[:, half, 0, :],
                h_scales[:, half, 0, :],
            )

        order_columns(W_E2)

        mask_f32 = keep.tile([P, HALVES, NODES], F32)
        nc.vector.tensor_copy(out=mask_f32[:], in_=mask_bf[:])
        degree = keep.tile([P, HALVES], F32)
        nc.vector.tensor_reduce(
            out=degree[:], in_=mask_f32[:], axis=mybir.AxisListType.X, op=ADD
        )
        running = []
        b2_all = psum.tile([P, H], F32, tag="bank")
        nc.tensor.matmul(out=b2_all[:], lhsT=ones[:], rhs=b2_row[:], start=True, stop=True)

        def start_sums():
            for half in range(HALVES):
                by_vector = sums.tile([P, H], F32, tag="by_vector")
                by_gpsimd = sums.tile([P, H], F32, tag="by_gpsimd")
                nc.vector.tensor_scalar(
                    out=by_gpsimd[:],
                    in0=b2_all[:],
                    scalar1=degree[:, half : half + 1],
                    scalar2=None,
                    op0=MULT,
                )
                running.append([by_vector, by_gpsimd])

        def add_h(half):
            by_gpsimd = running[half][1]
            nc.gpsimd.tensor_tensor(
                out=by_gpsimd[:], in0=by_gpsimd[:], in1=h_sb[:, half, :], op=ADD
            )

        def repeat_h():
            for plane in (h_codes, h_scales):
                nc.vector.tensor_copy(
                    out=plane[:, :, 1, :].bitcast(I32), in_=plane[:, :, 0, :].bitcast(I32)
                )

        source_term = {}

        def nodes_of(half):
            return h_codes[:, half, 0, :], h_scales[:, half, 0, :]

        def nodes_twice(half):
            return (
                h_codes[:, half].rearrange("p r c -> p (r c)"),
                h_scales[:, half].rearrange("p r c -> p (r c)"),
            )

        source_rows = {}

        def make_source_rows(half):
            product = psum.tile([P, H], F32, tag="bank")
            mx_pass(product[:], nodes_of(half), (w_words[:, W_XJ, :], w_planes[:, W_XJ, :]), True, True)
            rows = keep.tile([P, H], F32, name="source_rows%d" % half)
            nc.scalar.copy(out=rows[:], in_=product[:])
            source_rows[half] = rows

        def flip_source_rows(half):
            a_j = psum.tile([P, PACK, P], F32, tag="bank")
            for t in range(PACK):
                nc.tensor.transpose(a_j[:, t, :], source_rows[half][:, t:H:PACK], ident[:])
            return a_j

        def make_source_term(half, a_j):
            table = keep.tile([P, 2, P, 2], F32, name="source_term%d" % half)
            for d in range(2):
                nc.vector.tensor_tensor(
                    out=table[:, d].rearrange("p (j b) v -> p j b v", b=GRAPHS_PER_HALF),
                    in0=a_j[:, 2 * d : 2 * d + 2, :].rearrange(
                        "p v (b j) -> p j b v", b=GRAPHS_PER_HALF
                    ),
                    in1=b1[:, 2 * d : 2 * d + 2]
                    .unsqueeze(1)
                    .unsqueeze(1)
                    .to_broadcast([P, NODES, GRAPHS_PER_HALF, 2]),
                    op=ADD,
                )
            source_term[half] = table


        def half_and_j(pair):
            half, in_half = divmod(pair, PAIRS_PER_HALF)
            return half, in_half * PAIR

        def first_layer(pair, e_codes, e_scales):
            half, j = half_and_j(pair)
            p_bf = work.tile([P, 2, PAIR * P, 2], BF16, tag="p_bf")
            p_rounded[pair] = p_bf
            runs = PAIR * GRAPHS_PER_HALF
            for d in range(2):
                pre = psum.tile([P, 2, PAIR * P], F32, tag="bank")
                for v in range(2):
                    t = 2 * d + v
                    mx_pass(pre[:, v, :], channels(W_E2, t), (e_codes, e_scales), True, False)
                    mx_pass(pre[:, v, :], channels(W_XI, t), nodes_twice(half), False, True)
                nc.vector.tensor_tensor(
                    out=p_bf[:, d].rearrange("p (g i) v -> p g i v", g=runs),
                    in0=pre[:].rearrange("p v (g i) -> p g i v", g=runs),
                    in1=source_term[half][:, d, j * GRAPHS_PER_HALF : (j + PAIR) * GRAPHS_PER_HALF, :]
                    .unsqueeze(2)
                    .to_broadcast([P, runs, NODES, 2]),
                    op=ADD,
                )

        def relu(pair, grouped):
            p_bf = p_rounded[pair][:].rearrange("p d c v -> p c d v")
            r = grouped.rearrange("p c (d v) -> p c d v", d=2)
            nc.scalar.activation(out=r, in_=p_bf, func=RELU)

        def first_layer_of_last_pair(s, e_codes, e_scales):
            half, j = half_and_j(LAST_PAIR)
            p_bf = keep.tile([P, 2, P, 2], BF16, name="last_p%d" % s)
            r = keep.tile([P, P, PACK], BF16, name="last_r%d" % s, align_bytes=64)
            sources = slice((j + s) * GRAPHS_PER_HALF, (j + s + 1) * GRAPHS_PER_HALF)
            pre = psum.tile([P, PACK, P], F32, tag="bank")
            for t in range(PACK):
                mx_pass(pre[:, t, :], channels(W_E2, t), (e_codes, e_scales), True, False)
                mx_pass(pre[:, t, :], channels(W_XI, t), nodes_of(half), False, True)
            for d in range(2):
                nc.vector.tensor_tensor(
                    out=p_bf[:, d].rearrange("p (b i) v -> p b i v", b=GRAPHS_PER_HALF),
                    in0=pre[:, 2 * d : 2 * d + 2, :].rearrange(
                        "p v (b i) -> p b i v", b=GRAPHS_PER_HALF
                    ),
                    in1=source_term[half][:, d, sources, :]
                    .unsqueeze(2)
                    .to_broadcast([P, GRAPHS_PER_HALF, NODES, 2]),
                    op=ADD,
                )
            nc.scalar.activation(
                out=r[:].rearrange("p c (d v) -> p c d v", d=2),
                in_=p_bf[:].rearrange("p d c v -> p c d v"),
                func=RELU,
            )
            return r

        def quantise_last(s, r):
            codes = keep.tile([P, P], U32, name="last_codes%d" % s, align_bytes=64)
            scales = keep.tile([P, P], U8, name="last_scales%d" % s, align_bytes=64)
            quantise(r[:].rearrange("p c t -> p (c t)"), codes[:], scales[:])
            return codes[:], scales[:]

        def second_layer_pass(r):
            message = psum.tile([P, H], F32, tag="bank")
            mx_pass(message[:], r, (w_words[:, W_M2, :], w_planes[:, W_M2, :]), True, True)
            return message

        def mask_and_add_on_vector(message, half, j):
            by_vector = running[half][0]
            if j == 1:
                nc.vector.tensor_scalar(
                    out=by_vector[:],
                    in0=message[:],
                    scalar1=mask_f32[:, half, j : j + 1],
                    scalar2=None,
                    op0=MULT,
                )
                return
            nc.vector.scalar_tensor_tensor(
                out=by_vector[:],
                in0=message[:],
                scalar=mask_f32[:, half, j : j + 1],
                in1=by_vector[:],
                op0=MULT,
                op1=ADD,
            )

        def mask_on_scalar_add_on_gpsimd(message, half, j):
            by_gpsimd = running[half][1]
            masked = work.tile([P, H], F32, tag="masked")
            nc.scalar.activation(
                out=masked[:], in_=message[:], func=COPY, scale=mask_f32[:, half, j : j + 1]
            )
            nc.gpsimd.tensor_tensor(out=by_gpsimd[:], in0=by_gpsimd[:], in1=masked[:], op=ADD)

        def join_and_store(half, engine, cols):
            by_vector, by_gpsimd = running[half]
            engine.tensor_tensor(
                out=by_gpsimd[:, cols], in0=by_gpsimd[:, cols], in1=by_vector[:, cols], op=ADD
            )
            nc.sync.dma_start(
                out=out_rows[half * P : (half + 1) * P, cols], in_=by_gpsimd[:, cols]
            )

        E_PART = 0
        R_PART = 1

        def is_pair(pair):
            return 0 <= pair < PAIRS

        def e_run(pair):
            if pair < E_LEAD:
                return [pair]
            return [q for q in (pair, pair + 1) if pair % 2 == 0 and pair > E_LEAD and is_pair(q)]

        e_flipped = {}

        def flip_e(pair):
            e_flipped[pair] = flip_input_pair(e_blocks[pair * PAIR : (pair + 1) * PAIR])

        def group_e(step):
            group_words(e_flipped[step + E_LEAD], grouped_in[step][:, E_PART])

        grouped_in = {}
        quantised_in = {}
        p_rounded = {}

        def new_grouped(step):
            grouped = work.tile([P, 2, PAIR * P, PACK], BF16, tag="grouped", align_bytes=64)
            grouped_in[step] = grouped

        def quantise_grouped(step):
            parts = slice(
                E_PART if is_pair(step + E_LEAD) else R_PART,
                R_PART + 1 if is_pair(step - 1) else R_PART,
            )
            codes = work.tile([P, 2, PAIR * P], U32, tag="codes", bufs=E_LEAD + 1, align_bytes=64)
            scales = work.tile([P, 2, PAIR * P], U8, tag="scales", bufs=E_LEAD + 1, align_bytes=64)
            quantise(
                grouped_in[step][:, parts].rearrange("p k c t -> p (k c t)"),
                codes[:, parts, :].rearrange("p k c -> p (k c)"),
                scales[:, parts, :].rearrange("p k c -> p (k c)"),
            )
            quantised_in[step] = (codes, scales)

        def second_layer(pair):
            half, j = half_and_j(pair)
            codes, scales = quantised_in[pair + 1]
            messages = []
            for s in range(PAIR):
                cols = slice(s * P, (s + 1) * P)
                messages.append(second_layer_pass((codes[:, R_PART, cols], scales[:, R_PART, cols])))
            mask_on_scalar_add_on_gpsimd(messages[0], half, j)
            mask_and_add_on_vector(messages[1], half, j + 1)

        make_source_rows(0)
        repeat_h()
        order_columns(W_XI)
        start_sums()
        for step in range(-E_LEAD, LAST_PAIR):
            for pair in e_run(step + E_LEAD):
                flip_e(pair)
            if step - 1 in grouped_in:
                quantise_grouped(step - 1)
            new_grouped(step)
            if is_pair(step + E_LEAD) and step != 0:
                group_e(step)
            if step == -E_LEAD:
                source_columns = flip_source_rows(0)
            if step == 1 - E_LEAD:
                make_source_term(0, source_columns)
            if is_pair(step - 3):
                second_layer(step - 3)
                if step - 3 in (0, 2):
                    add_h((step - 3) // 2)
                if step - 3 == PAIRS_PER_HALF + 2:
                    join_and_store(0, nc.gpsimd, slice(0, H))
            if is_pair(step - 1):
                relu(step - 1, grouped_in[step][:, R_PART])
            if is_pair(step):
                codes, scales = quantised_in[step - E_LEAD]
                first_layer(step, codes[:, E_PART, :], scales[:, E_PART, :])
                if step == 0:
                    flip_e(E_LEAD)
                    flip_e(E_LEAD + 1)
                    group_e(0)
                if step == PAIRS_PER_HALF // 2:
                    make_source_rows(1)
                if step == PAIRS_PER_HALF // 2 + 1:
                    make_source_term(1, flip_source_rows(1))

        codes, scales = quantised_in[LAST_PAIR - E_LEAD]
        quantise_grouped(LAST_PAIR - 1)
        second_layer(LAST_PAIR - 3)
        new_grouped(LAST_PAIR)
        relu(LAST_PAIR - 1, grouped_in[LAST_PAIR][:, R_PART])
        first, second = (slice(s * P, (s + 1) * P) for s in range(PAIR))
        r_first = first_layer_of_last_pair(0, codes[:, E_PART, first], scales[:, E_PART, first])
        quantise_grouped(LAST_PAIR)
        second_layer(LAST_PAIR - 2)
        r_second = first_layer_of_last_pair(1, codes[:, E_PART, second], scales[:, E_PART, second])
        first_quantised = quantise_last(0, r_first)
        second_layer(LAST_PAIR - 1)
        half, j = half_and_j(LAST_PAIR)
        message = second_layer_pass(first_quantised)
        second_quantised = quantise_last(1, r_second)
        mask_and_add_on_vector(message, half, j)
        mask_and_add_on_vector(second_layer_pass(second_quantised), half, j + 1)
        for piece in range(2):
            join_and_store(half, nc.vector, slice(piece * H // 2, (piece + 1) * H // 2))
